import numpy as np
import ml_dtypes


def mxq(x, axis, fmt="e4m3"):
    dtype, down = {"e4m3": (ml_dtypes.float8_e4m3fn, 7), "e5m2": (ml_dtypes.float8_e5m2, 14)}[fmt]
    v = np.moveaxis(np.asarray(x, np.float32).astype(ml_dtypes.bfloat16).astype(np.float64), axis, -1)
    blocks = v.reshape(v.shape[:-1] + (-1, 32))
    amax = np.abs(blocks).max(-1, keepdims=True)
    byte = np.maximum(np.where(amax > 0, np.frexp(amax)[1] - 1 + 127, 0) - down, 1)
    scale = np.exp2(byte - 127.0)
    codes = (blocks / scale).astype(np.float32).astype(dtype).astype(np.float64)
    return np.moveaxis((codes * scale).reshape(v.shape), -1, axis)


WIDE = False


def mx_kscale(k):
    if not WIDE:
        return np.ones(k)
    levels = np.array([10, -10, 5, -5, 0])
    a = np.random.permutation(np.resize(levels, k // 512 * 4)).reshape(k // 512, 4)
    idx = np.arange(k)
    return np.exp2(a[idx // 512, idx % 128 // 32])


BF16 = ml_dtypes.bfloat16


def bf(x):
    return np.asarray(x, np.float32).astype(BF16)


def f64(x):
    return np.asarray(x).astype(np.float64)


E2M1 = np.array([0.0, 0.5, 1.0, 1.5, 2.0, 3.0, 4.0, 6.0, -0.0, -0.5, -1.0, -1.5, -2.0, -3.0, -4.0, -6.0])


def pack_weight(w, fmt):
    k, n = w.shape
    w = f64(bf(w)).reshape(k // 32, 32, n)
    amax = np.abs(w).max(1)
    if fmt == "e4m3":
        byte = np.frexp(amax)[1] - 1 + 127 - 7
    else:
        mant, ex = np.frexp(amax / 6.0)
        byte = np.where(mant > 0.5, ex, ex - 1) + 127
    byte = np.clip(np.where(amax > 0, byte, 1), 1, 254)
    scaled = (w * np.exp2(127.0 - byte)[:, None, :]).reshape(k, n).astype(np.float32)
    by_word = np.ascontiguousarray(scaled.reshape(k // 512, 128, 4, n).transpose(0, 1, 3, 2))
    if fmt == "e4m3":
        words = by_word.astype(ml_dtypes.float8_e4m3fn).view(np.uint8)
    else:
        c = by_word.astype(ml_dtypes.float4_e2m1fn).view(np.uint8) & 0xF
        words = c[..., 0::2] | (c[..., 1::2] << 4)
    return np.ascontiguousarray(words), np.ascontiguousarray(byte.astype(np.uint8).reshape(k // 512, 16, n))


def unpack_weight(words, scales, fmt):
    g, p, n, _ = words.shape
    if fmt == "e4m3":
        vals = np.ascontiguousarray(words).view(ml_dtypes.float8_e4m3fn).astype(np.float64)
    else:
        nib = np.empty((g, p, n, 4), np.uint8)
        nib[..., 0::2] = words & 0xF
        nib[..., 1::2] = words >> 4
        vals = E2M1[nib]
    vals = vals * np.repeat(np.exp2(scales.astype(np.float64) - 127.0), 8, axis=1)[..., None]
    return vals.transpose(0, 1, 3, 2).reshape(g * 512, n)

def pack4(w):
    words, scales = pack_weight(w, "e2m1")
    return words.reshape(words.shape[0], 128, -1), scales


def unpack4(words, scales):
    return unpack_weight(words.reshape(words.shape[0], 128, -1, 2), scales, "e2m1")


B, N, DIM, H, DH = 2, 256, 1536, 16, 96
D1 = DH // 3


def rotate_half(t):
    d = t.shape[-1]
    t1, t2 = t[..., : (d + 1) // 2], t[..., (d + 1) // 2:]
    return np.concatenate((-t2, t1), axis=-1)


def apply_rope(t, freqs):
    return t * np.cos(freqs) + rotate_half(t) * np.sin(freqs)


def rope3(t, fs):
    return np.concatenate([apply_rope(ts, f) for ts, f in zip(np.split(t, (D1, 2 * D1), axis=-1), fs)], axis=-1)


def setup_inputs():
    s = mx_kscale(DIM)
    x = bf(np.random.standard_normal((B, N, DIM)) * s)
    f1 = bf(np.random.uniform(0.0, 1.0, (N, D1)))
    f2 = bf(np.random.uniform(0.0, 1.0, (N, D1)))
    f3 = bf(np.random.uniform(0.0, 1.0, (N, D1)))
    words, scales = pack4(np.random.standard_normal((DIM, 3 * H * DH)) / np.sqrt(DIM) / s[:, None])
    return {"x": x, "f1": f1, "f2": f2, "f3": f3, "Wqkv_words": words, "Wqkv_scales": scales}


def reference(x, f1, f2, f3, Wqkv_words, Wqkv_scales):
    qkv = mxq(f64(x), 2, "e4m3") @ unpack4(Wqkv_words, Wqkv_scales)
    q, k, v = np.split(qkv, 3, axis=-1)
    to_heads = lambda t: t.reshape(B, N, H, DH).transpose(0, 2, 1, 3)
    q, k, v = to_heads(q), to_heads(k), to_heads(v)
    fs = (f64(f1), f64(f2), f64(f3))
    return rope3(q, fs), rope3(k, fs), v

@@ -1,0 +1,231 @@
+from contextlib import ExitStack
+
+import concourse.mybir as mybir
+from concourse.masks import make_identity
+
+F32 = mybir.dt.float32
+BF16 = mybir.dt.bfloat16
+I32 = mybir.dt.int32
+U32 = mybir.dt.uint32
+U8 = mybir.dt.uint8
+FP8X4 = mybir.dt.float8_e4m3fn_x4
+FP4X4 = mybir.dt.float4_e2m1fn_x4
+ACT = mybir.ActivationFunctionType
+ALU = mybir.AluOpType
+
+P = 128
+BATCH, TOKENS, DIM = 2, 256, 1536
+HEADS, HEAD = 16, 96
+THIRD = HEADS * HEAD
+HALF = 16
+K_PASS = 512
+PASSES = DIM // K_PASS
+TOK = 4
+PAIRS = TOKENS // TOK
+N_PASS = 128
+UNIT_HEADS = 4
+UNIT = UNIT_HEADS * HEAD
+BANKS = UNIT // N_PASS
+UNITS = THIRD // UNIT
+LOAD = 2 * UNIT
+
+FLOPS = 2 * BATCH * TOKENS * DIM * 3 * THIRD
+
+
+def load_inputs(nc, keep, x, angles, w_words_in, w_scales_in):
+    w_scales = keep.tile([P, PASSES, 3 * THIRD], U8, align_bytes=64)
+    nc.vector.memset(w_scales[:].bitcast(I32), 0)
+
+    x_sb = keep.tile([P, TOK, DIM], BF16)
+    for j in range(0, TOK, 2):
+        for b in range(BATCH):
+            nc.scalar.dma_start(
+                out=x_sb[b:P:BATCH, j : j + 2, :],
+                in_=x[b].rearrange("(p j) k -> p j k", j=TOK)[:, j : j + 2, :],
+            )
+
+    f_sb = keep.tile([P, 3, TOK * 2 * HALF], BF16)
+    for a in range(3):
+        nc.gpsimd.dma_start(
+            out=f_sb[:, a, :],
+            in_=angles[a]
+            .rearrange("(p j) c -> p (j c)", j=TOK)
+            .unsqueeze(1)
+            .to_broadcast([PAIRS, BATCH, TOK * 2 * HALF]),
+        )
+
+    words_i32 = w_words_in.bitcast(I32).rearrange("g p n -> p g n")
+    scales_i32 = w_scales_in.bitcast(I32).rearrange("g q n -> q g n")
+    w_words = {}
+
+    def load_words(n):
+        w_words[n] = keep.tile([P, PASSES, 2 * LOAD], U8, align_bytes=64, name="w_words%d" % n)
+        nc.sync.dma_start(
+            out=w_words[n][:].bitcast(I32),
+            in_=words_i32[:, :, n * LOAD // 2 : (n + 1) * LOAD // 2],
+        )
+
+    load_words(0)
+    for b in range(2):
+        for r in range(4):
+            nc.sync.dma_start(
+                out=w_scales[:].bitcast(I32)[32 * b + r : P : 64, :, :],
+                in_=scales_i32[4 * b + r : 16 : 8, :, :],
+            )
+    for half in range(2):
+        for third in range(3):
+            if (half, third) != (0, 0):
+                load_words(2 * third + half)
+    return x_sb, f_sb, w_words, w_scales
+
+
+def rope_tables(nc, keep, f_sb):
+    by_token = f_sb[:].rearrange("p a (j c) -> p j a c", j=TOK)
+    half_sin = keep.tile([P, TOK, 3, 2 * HALF], F32)
+    nc.scalar.activation(out=half_sin[:], in_=by_token, func=ACT.Sin, scale=0.5)
+    squared = keep.tile([P, TOK, HEAD], F32)
+    nc.scalar.activation(
+        out=squared[:], in_=half_sin[:].rearrange("p j a c -> p j (a c)"), func=ACT.Square
+    )
+    cos2 = keep.tile([P, TOK, 2, HEAD], F32)
+    nc.scalar.activation(
+        out=cos2[:],
+        in_=squared[:].unsqueeze(2).to_broadcast([P, TOK, 2, HEAD]),
+        func=ACT.Copy,
+        scale=-2.0,
+        bias=1.0,
+    )
+    signed_sin = keep.tile([P, TOK, 3, 2, HALF], F32)
+    halves = by_token.rearrange("p j a (h i) -> p j a h i", h=2)
+    for h in range(2):
+        nc.scalar.activation(
+            out=signed_sin[:, :, :, h, :],
+            in_=halves[:, :, :, h, :],
+            func=ACT.Sin,
+            scale=(-1.0 if h == 0 else 1.0),
+        )
+    sin2 = keep.tile([P, TOK, 2, HEAD], F32)
+    nc.scalar.copy(
+        out=sin2[:],
+        in_=signed_sin[:]
+        .rearrange("p j a h i -> p j (a h i)")
+        .unsqueeze(2)
+        .to_broadcast([P, TOK, 2, HEAD]),
+    )
+    return (
+        cos2[:].rearrange("p j r d -> p j (r d)"),
+        sin2[:].rearrange("p j r d -> p j (r d)"),
+    )
+
+
+def quantise_x(nc, keep, psum, x_sb):
+    ident = keep.tile([P, P], F32)
+    make_identity(nc, ident[:])
+    tiles = TOK * PASSES
+    grouped = keep.tile([P, tiles, 4 * P], BF16, align_bytes=64)
+    x_codes = keep.tile([P, tiles, P], U32, align_bytes=64)
+    x_scales = keep.tile([P, tiles, P], U8, align_bytes=64)
+    for m in range(0, tiles, 2):
+        flipped = psum.tile([P, 4, P], F32, tag="bank")
+        for a in range(2):
+            j, g = divmod(m + a, PASSES)
+            words = x_sb[:, j, :].bitcast(F32)
+            for u in range(2):
+                nc.tensor.transpose(
+                    flipped[:, 2 * a + u, :],
+                    words[:, 256 * g + u : 256 * (g + 1) : 2],
+                    ident[:],
+                )
+        side_by_side = grouped[:, m : m + 2, :].bitcast(F32).rearrange("p a (r u) -> p a r u", u=2)
+        pairs = flipped[:].rearrange("p (a u) r -> p a r u", u=2)
+        if m % 4 == 0:
+            nc.vector.tensor_copy(out=side_by_side, in_=pairs)
+        else:
+            nc.scalar.copy(out=side_by_side, in_=pairs)
+        nc.vector.quantize_mx(
+            out=x_codes[:, m : m + 2, :].rearrange("p a r -> p (a r)").bitcast(FP8X4),
+            scales=x_scales[:, m : m + 2, :].rearrange("p a r -> p (a r)"),
+            in_=grouped[:, m : m + 2, :].rearrange("p a c -> p (a c)"),
+        )
+    return x_codes, x_scales
+
+
+def tile_attention_pa_kernel(
+    tc, x, f1, f2, f3, Wqkv_words, Wqkv_scales, out_0, out_1, out_2
+):
+    nc = tc.nc
+    outs = (out_0, out_1, out_2)
+    with ExitStack() as ctx:
+        keep = ctx.enter_context(tc.tile_pool(name="keep", bufs=1))
+        work = ctx.enter_context(tc.tile_pool(name="work", bufs=3))
+        psum = ctx.enter_context(tc.psum_pool(name="psum", bufs=8))
+
+        x_sb, f_sb, w_words, w_scales = load_inputs(
+            nc, keep, x, (f1, f2, f3), Wqkv_words, Wqkv_scales
+        )
+        x_codes, x_scales = quantise_x(nc, keep, psum, x_sb)
+        cos2, sin2 = rope_tables(nc, keep, f_sb)
+
+        for unit in range(UNITS):
+            for third in range(3):
+                first_col = third * THIRD + unit * UNIT
+                words = w_words[first_col // LOAD]
+                result = work.tile([P, UNIT_HEADS, TOK, HEAD], F32, tag="result")
+                if third < 2:
+                    with_cos = work.tile([P, TOK, UNIT], F32, tag="with_cos")
+                    with_sin = work.tile([P, TOK, UNIT], F32, tag="with_sin")
+                for s in range(BANKS):
+                    col = first_col + s * N_PASS
+                    in_load = col % LOAD
+                    acc = psum.tile([P, TOK, N_PASS], F32, tag="bank")
+                    for j in range(TOK):
+                        for g in range(PASSES):
+                            nc.tensor.matmul_mx(
+                                out=acc[:, j, :],
+                                lhsT=x_codes[:, PASSES * j + g, :].bitcast(FP8X4),
+                                lhsT_scale=x_scales[:, PASSES * j + g, :],
+                                rhs=words[:, g, 2 * in_load : 2 * (in_load + N_PASS)].bitcast(FP4X4),
+                                rhs_scale=w_scales[:, g, col : col + N_PASS],
+                                start=(g == 0),
+                                stop=(g == PASSES - 1),
+                            )
+                    begin = 2 * HALF * s
+                    if third < 2:
+                        here = slice(s * N_PASS, (s + 1) * N_PASS)
+                        window = slice(begin, begin + N_PASS)
+                        nc.vector.tensor_tensor(
+                            out=with_cos[:, :, here], in0=acc[:], in1=cos2[:, :, window], op=ALU.mult
+                        )
+                        split = "p j (m h i) -> p j m h i"
+                        acc_h = acc[:].rearrange(split, h=2, i=HALF)
+                        sin_h = sin2[:, :, window].rearrange(split, h=2, i=HALF)
+                        out_h = with_sin[:, :, here].rearrange(split, h=2, i=HALF)
+                        for h in range(2):
+                            nc.vector.tensor_tensor(
+                                out=out_h[:, :, :, h, :],
+                                in0=acc_h[:, :, :, 1 - h, :],
+                                in1=sin_h[:, :, :, h, :],
+                                op=ALU.mult,
+                            )
+                    else:
+                        rest = HEAD - begin
+                        nc.scalar.copy(out=result[:, s, :, begin:HEAD], in_=acc[:, :, 0:rest])
+                        nc.scalar.copy(
+                            out=result[:, s + 1, :, 0 : N_PASS - rest], in_=acc[:, :, rest:N_PASS]
+                        )
+                if third < 2:
+                    by_head = "p j (h d) -> p j h d"
+                    nc.gpsimd.tensor_tensor(
+                        out=result[:].rearrange("p h j d -> p j h d"),
+                        in0=with_cos[:].rearrange(by_head, d=HEAD),
+                        in1=with_sin[:].rearrange(by_head, d=HEAD),
+                        op=ALU.add,
+                    )
+                head = unit * UNIT_HEADS
+                for b in range(BATCH):
+                    nc.sync.dma_start(
+                        out=outs[third][b, head : head + UNIT_HEADS].rearrange(
+                            "h (p j) d -> p h (j d)", j=TOK
+                        ),
+                        in_=result[b:P:BATCH].rearrange("p h j d -> p h (j d)"),
+                    )

@@ -22,12 +22,14 @@ K_PASS = 512
 PASSES = DIM // K_PASS
 TOK = 4
 PAIRS = TOKENS // TOK
-N_PASS = 128
-UNIT_HEADS = 4
+
+UNIT_HEADS = 8
 UNIT = UNIT_HEADS * HEAD
-BANKS = UNIT // N_PASS
-UNITS = THIRD // UNIT
-LOAD = 2 * UNIT
+WIDE = 512
+NARROW = UNIT - WIDE
+WIDE_HEADS = WIDE // HEAD
+LATE_HEADS = UNIT_HEADS - WIDE_HEADS
+PERIODS = 6
 
 FLOPS = 2 * BATCH * TOKENS * DIM * 3 * THIRD
 
@@ -36,17 +38,9 @@ def load_inputs(nc, keep, x, angles, w_words_in, w_scales_in):
     w_scales = keep.tile([P, PASSES, 3 * THIRD], U8, align_bytes=64)
     nc.vector.memset(w_scales[:].bitcast(I32), 0)
 
-    x_sb = keep.tile([P, TOK, DIM], BF16)
-    for j in range(0, TOK, 2):
-        for b in range(BATCH):
-            nc.scalar.dma_start(
-                out=x_sb[b:P:BATCH, j : j + 2, :],
-                in_=x[b].rearrange("(p j) k -> p j k", j=TOK)[:, j : j + 2, :],
-            )
-
     f_sb = keep.tile([P, 3, TOK * 2 * HALF], BF16)
     for a in range(3):
-        nc.gpsimd.dma_start(
+        nc.sync.dma_start(
             out=f_sb[:, a, :],
             in_=angles[a]
             .rearrange("(p j) c -> p (j c)", j=TOK)
@@ -54,46 +48,40 @@ def load_inputs(nc, keep, x, angles, w_words_in, w_scales_in):
             .to_broadcast([PAIRS, BATCH, TOK * 2 * HALF]),
         )
 
+    by_partition = x.rearrange("b (p j) k -> p b (j k)", j=TOK)
+    x_sb = []
+    for j in range(0, TOK, 2):
+        two_tokens = keep.tile([P, 2, DIM], BF16, name="x_sb%d" % j)
+        nc.scalar.dma_start(
+            out=two_tokens[:].rearrange("p j k -> p (j k)"),
+            in_=by_partition[:, :, j * DIM : (j + 2) * DIM],
+        )
+        x_sb.append(two_tokens)
+
     words_i32 = w_words_in.bitcast(I32).rearrange("g p n -> p g n")
     scales_i32 = w_scales_in.bitcast(I32).rearrange("g q n -> q g n")
     w_words = {}
-
-    def load_words(n):
-        w_words[n] = keep.tile([P, PASSES, 2 * LOAD], U8, align_bytes=64, name="w_words%d" % n)
-        nc.sync.dma_start(
-            out=w_words[n][:].bitcast(I32),
-            in_=words_i32[:, :, n * LOAD // 2 : (n + 1) * LOAD // 2],
-        )
-
-    load_words(0)
-    for b in range(2):
-        for r in range(4):
-            nc.sync.dma_start(
-                out=w_scales[:].bitcast(I32)[32 * b + r : P : 64, :, :],
-                in_=scales_i32[4 * b + r : 16 : 8, :, :],
-            )
     for half in range(2):
         for third in range(3):
-            if (half, third) != (0, 0):
-                load_words(2 * third + half)
+            n = 2 * third + half
+            w_words[n] = keep.tile([P, PASSES, 2 * UNIT], U8, align_bytes=64, name="w_words%d" % n)
+            nc.sync.dma_start(
+                out=w_words[n][:].bitcast(I32),
+                in_=words_i32[:, :, n * UNIT // 2 : (n + 1) * UNIT // 2],
+            )
+            if n == 0:
+                for r in range(4):
+                    nc.sync.dma_start(
+                        out=w_scales[:].bitcast(I32)[r:P:32, :, :], in_=scales_i32[r:16:4, :, :]
+                    )
     return x_sb, f_sb, w_words, w_scales
 
 
 def rope_tables(nc, keep, f_sb):
     by_token = f_sb[:].rearrange("p a (j c) -> p j a c", j=TOK)
-    half_sin = keep.tile([P, TOK, 3, 2 * HALF], F32)
-    nc.scalar.activation(out=half_sin[:], in_=by_token, func=ACT.Sin, scale=0.5)
-    squared = keep.tile([P, TOK, HEAD], F32)
+    half_sin = keep.tile([P, TOK, HEAD], F32)
     nc.scalar.activation(
-        out=squared[:], in_=half_sin[:].rearrange("p j a c -> p j (a c)"), func=ACT.Square
-    )
-    cos2 = keep.tile([P, TOK, 2, HEAD], F32)
-    nc.scalar.activation(
-        out=cos2[:],
-        in_=squared[:].unsqueeze(2).to_broadcast([P, TOK, 2, HEAD]),
-        func=ACT.Copy,
-        scale=-2.0,
-        bias=1.0,
+        out=half_sin[:].rearrange("p j (a c) -> p j a c", a=3), in_=by_token, func=ACT.Sin, scale=0.5
     )
     signed_sin = keep.tile([P, TOK, 3, 2, HALF], F32)
     halves = by_token.rearrange("p j a (h i) -> p j a h i", h=2)
@@ -104,32 +92,52 @@ def rope_tables(nc, keep, f_sb):
             func=ACT.Sin,
             scale=(-1.0 if h == 0 else 1.0),
         )
-    sin2 = keep.tile([P, TOK, 2, HEAD], F32)
-    nc.scalar.copy(
-        out=sin2[:],
-        in_=signed_sin[:]
-        .rearrange("p j a h i -> p j (a h i)")
-        .unsqueeze(2)
-        .to_broadcast([P, TOK, 2, HEAD]),
-    )
+    squared = keep.tile([P, TOK, HEAD], F32)
+    nc.gpsimd.tensor_tensor(out=squared[:], in0=half_sin[:], in1=half_sin[:], op=ALU.mult)
+    cos_t = keep.tile([P, TOK, PERIODS, HEAD], F32)
+    sin_t = keep.tile([P, TOK, PERIODS, HEAD], F32)
+    one_period = signed_sin[:].rearrange("p j a h i -> p j (a h i)")
+    for j in range(TOK):
+        nc.gpsimd.tensor_scalar(
+            out=cos_t[:, j, :, :],
+            in0=squared[:, j, :].unsqueeze(1).to_broadcast([P, PERIODS, HEAD]),
+            scalar1=-2.0,
+            scalar2=1.0,
+            op0=ALU.mult,
+            op1=ALU.add,
+        )
+        nc.gpsimd.tensor_scalar(
+            out=sin_t[:, j, :, :],
+            in0=one_period[:, j, :].unsqueeze(1).to_broadcast([P, PERIODS, HEAD]),
+            scalar1=1.0,
+            scalar2=0.0,
+            op0=ALU.mult,
+            op1=ALU.add,
+        )
     return (
-        cos2[:].rearrange("p j r d -> p j (r d)"),
-        sin2[:].rearrange("p j r d -> p j (r d)"),
+        cos_t[:].rearrange("p j r d -> p j (r d)"),
+        sin_t[:].rearrange("p j r d -> p j (r d)"),
     )
 
 
-def quantise_x(nc, keep, psum, x_sb):
-    ident = keep.tile([P, P], F32)
-    make_identity(nc, ident[:])
+def quantise_x(nc, keep, psum, x_sb, ident):
     tiles = TOK * PASSES
     grouped = keep.tile([P, tiles, 4 * P], BF16, align_bytes=64)
     x_codes = keep.tile([P, tiles, P], U32, align_bytes=64)
     x_scales = keep.tile([P, tiles, P], U8, align_bytes=64)
+
+    def quantise(m):
+        nc.vector.quantize_mx(
+            out=x_codes[:, m : m + 2, :].rearrange("p a r -> p (a r)").bitcast(FP8X4),
+            scales=x_scales[:, m : m + 2, :].rearrange("p a r -> p (a r)"),
+            in_=grouped[:, m : m + 2, :].rearrange("p a c -> p (a c)"),
+        )
+
     for m in range(0, tiles, 2):
         flipped = psum.tile([P, 4, P], F32, tag="bank")
         for a in range(2):
             j, g = divmod(m + a, PASSES)
-            words = x_sb[:, j, :].bitcast(F32)
+            words = x_sb[j // 2][:, j % 2, :].bitcast(F32)
             for u in range(2):
                 nc.tensor.transpose(
                     flipped[:, 2 * a + u, :],
@@ -142,11 +150,9 @@ def quantise_x(nc, keep, psum, x_sb):
             nc.vector.tensor_copy(out=side_by_side, in_=pairs)
         else:
             nc.scalar.copy(out=side_by_side, in_=pairs)
-        nc.vector.quantize_mx(
-            out=x_codes[:, m : m + 2, :].rearrange("p a r -> p (a r)").bitcast(FP8X4),
-            scales=x_scales[:, m : m + 2, :].rearrange("p a r -> p (a r)"),
-            in_=grouped[:, m : m + 2, :].rearrange("p a c -> p (a c)"),
-        )
+        if m > 0:
+            quantise(m - 2)
+    quantise(tiles - 2)
     return x_codes, x_scales
 
 
@@ -157,75 +163,112 @@ def tile_attention_pa_kernel(
     outs = (out_0, out_1, out_2)
     with ExitStack() as ctx:
         keep = ctx.enter_context(tc.tile_pool(name="keep", bufs=1))
-        work = ctx.enter_context(tc.tile_pool(name="work", bufs=3))
+        scratch = ctx.enter_context(tc.tile_pool(name="scratch", bufs=2))
+        results = ctx.enter_context(tc.tile_pool(name="results", bufs=3))
         psum = ctx.enter_context(tc.psum_pool(name="psum", bufs=8))
 
+        ctx.enter_context(tc.manual_schedule())
+
+        ident = keep.tile([P, P], F32)
+        make_identity(nc, ident[:])
         x_sb, f_sb, w_words, w_scales = load_inputs(
             nc, keep, x, (f1, f2, f3), Wqkv_words, Wqkv_scales
         )
-        x_codes, x_scales = quantise_x(nc, keep, psum, x_sb)
-        cos2, sin2 = rope_tables(nc, keep, f_sb)
+        cos_t, sin_t = rope_tables(nc, keep, f_sb)
+        x_codes, x_scales = quantise_x(nc, keep, psum, x_sb, ident)
 
-        for unit in range(UNITS):
+        def project(n, j0, n_tok, c0, cols, n_pass):
+            acc = psum.tile([P, n_tok, cols], F32, tag="bank")
+            for t in range(n_tok):
+                for c in range(c0, c0 + cols, n_pass):
+                    for g in range(PASSES):
+                        nc.tensor.matmul_mx(
+                            out=acc[:, t, c - c0 : c - c0 + n_pass],
+                            lhsT=x_codes[:, PASSES * (j0 + t) + g, :].bitcast(FP8X4),
+                            lhsT_scale=x_scales[:, PASSES * (j0 + t) + g, :],
+                            rhs=w_words[n][:, g, 2 * c : 2 * (c + n_pass)].bitcast(FP4X4),
+                            rhs_scale=w_scales[:, g, n * UNIT + c : n * UNIT + c + n_pass],
+                            start=(g == 0),
+                            stop=(g == PASSES - 1),
+                        )
+            return acc
+
+        def products(acc, with_cos, with_sin, j0, n_tok, c0, cols):
+            toks = slice(j0, j0 + n_tok)
+            here = slice(c0, c0 + cols)
+            window = slice(c0 % HEAD, c0 % HEAD + cols)
+            nc.vector.tensor_tensor(
+                out=with_cos[:, toks, here], in0=acc[:], in1=cos_t[:, toks, window], op=ALU.mult
+            )
+            split = "p j (m h i) -> p j m h i"
+            acc_h = acc[:].rearrange(split, h=2, i=HALF)
+            sin_h = sin_t[:, toks, window].rearrange(split, h=2, i=HALF)
+            out_h = with_sin[:, toks, here].rearrange(split, h=2, i=HALF)
+            for h in range(2):
+                nc.vector.tensor_tensor(
+                    out=out_h[:, :, :, h, :],
+                    in0=acc_h[:, :, :, 1 - h, :],
+                    in1=sin_h[:, :, :, h, :],
+                    op=ALU.mult,
+                )
+
+        def add_products(result, with_cos, with_sin, c0, cols):
+            by_head = "p j (h d) -> p j h d"
+            nc.gpsimd.tensor_tensor(
+                out=result[:].rearrange("p h j d -> p j h d"),
+                in0=with_cos[:, :, c0 : c0 + cols].rearrange(by_head, d=HEAD),
+                in1=with_sin[:, :, c0 : c0 + cols].rearrange(by_head, d=HEAD),
+                op=ALU.add,
+            )
+
+        def store(result, third, head, n_heads):
+            for b in range(BATCH):
+                nc.sync.dma_start(
+                    out=outs[third][b, head : head + n_heads].rearrange(
+                        "h (p j) d -> p h (j d)", j=TOK
+                    ),
+                    in_=result[b:P:BATCH].rearrange("p h j d -> p h (j d)"),
+                )
+
+        cut = WIDE_HEADS * HEAD
+        over = WIDE - cut
+        for half in range(2):
             for third in range(3):
-                first_col = third * THIRD + unit * UNIT
-                words = w_words[first_col // LOAD]
-                result = work.tile([P, UNIT_HEADS, TOK, HEAD], F32, tag="result")
-                if third < 2:
-                    with_cos = work.tile([P, TOK, UNIT], F32, tag="with_cos")
-                    with_sin = work.tile([P, TOK, UNIT], F32, tag="with_sin")
-                for s in range(BANKS):
-                    col = first_col + s * N_PASS
-                    in_load = col % LOAD
-                    acc = psum.tile([P, TOK, N_PASS], F32, tag="bank")
-                    for j in range(TOK):
-                        for g in range(PASSES):
-                            nc.tensor.matmul_mx(
-                                out=acc[:, j, :],
-                                lhsT=x_codes[:, PASSES * j + g, :].bitcast(FP8X4),
-                                lhsT_scale=x_scales[:, PASSES * j + g, :],
-                                rhs=words[:, g, 2 * in_load : 2 * (in_load + N_PASS)].bitcast(FP4X4),
-                                rhs_scale=w_scales[:, g, col : col + N_PASS],
-                                start=(g == 0),
-                                stop=(g == PASSES - 1),
-                            )
-                    begin = 2 * HALF * s
-                    if third < 2:
-                        here = slice(s * N_PASS, (s + 1) * N_PASS)
-                        window = slice(begin, begin + N_PASS)
-                        nc.vector.tensor_tensor(
-                            out=with_cos[:, :, here], in0=acc[:], in1=cos2[:, :, window], op=ALU.mult
-                        )
-                        split = "p j (m h i) -> p j m h i"
-                        acc_h = acc[:].rearrange(split, h=2, i=HALF)
-                        sin_h = sin2[:, :, window].rearrange(split, h=2, i=HALF)
-                        out_h = with_sin[:, :, here].rearrange(split, h=2, i=HALF)
-                        for h in range(2):
-                            nc.vector.tensor_tensor(
-                                out=out_h[:, :, :, h, :],
-                                in0=acc_h[:, :, :, 1 - h, :],
-                                in1=sin_h[:, :, :, h, :],
-                                op=ALU.mult,
-                            )
+                n = 2 * third + half
+                head = half * UNIT_HEADS
+                rope = third < 2
+                early = results.tile([P, WIDE_HEADS, TOK, HEAD], F32, tag="early")
+                late = results.tile([P, LATE_HEADS, TOK, HEAD], F32, tag="late")
+                if rope:
+                    with_cos = scratch.tile([P, TOK, UNIT], F32, tag="with_cos")
+                    with_sin = scratch.tile([P, TOK, UNIT], F32, tag="with_sin")
+                for j in range(TOK):
+                    acc = project(n, j, 1, 0, WIDE, WIDE)
+                    if rope:
+                        products(acc, with_cos, with_sin, j, 1, 0, WIDE)
                     else:
-                        rest = HEAD - begin
-                        nc.scalar.copy(out=result[:, s, :, begin:HEAD], in_=acc[:, :, 0:rest])
                         nc.scalar.copy(
-                            out=result[:, s + 1, :, 0 : N_PASS - rest], in_=acc[:, :, rest:N_PASS]
+                            out=early[:, :, j, :],
+                            in_=acc[:, 0, 0:cut].rearrange("p (h d) -> p h d", d=HEAD),
                         )
-                if third < 2:
-                    by_head = "p j (h d) -> p j h d"
-                    nc.gpsimd.tensor_tensor(
-                        out=result[:].rearrange("p h j d -> p j h d"),
-                        in0=with_cos[:].rearrange(by_head, d=HEAD),
-                        in1=with_sin[:].rearrange(by_head, d=HEAD),
-                        op=ALU.add,
-                    )
-                head = unit * UNIT_HEADS
-                for b in range(BATCH):
-                    nc.sync.dma_start(
-                        out=outs[third][b, head : head + UNIT_HEADS].rearrange(
-                            "h (p j) d -> p h (j d)", j=TOK
-                        ),
-                        in_=result[b:P:BATCH].rearrange("p h j d -> p h (j d)"),
-                    )
+                        nc.scalar.copy(out=late[:, 0, j, 0:over], in_=acc[:, 0, cut:WIDE])
+                if rope:
+                    add_products(early, with_cos, with_sin, 0, cut)
+                store(early, third, head, WIDE_HEADS)
+                for j in range(0, TOK, 2):
+                    acc = project(n, j, 2, WIDE, NARROW, 128)
+                    if rope:
+                        products(acc, with_cos, with_sin, j, 2, WIDE, NARROW)
+                    else:
+                        nc.scalar.copy(
+                            out=late[:, 0, j : j + 2, over:HEAD], in_=acc[:, :, 0 : HEAD - over]
+                        )
+                        nc.scalar.copy(
+                            out=late[:, 1:LATE_HEADS, j : j + 2, :].rearrange("p h j d -> p j h d"),
+                            in_=acc[:, :, HEAD - over : NARROW].rearrange(
+                                "p j (h d) -> p j h d", d=HEAD
+                            ),
+                        )
+                if rope:
+                    add_products(late, with_cos, with_sin, cut, UNIT - cut)
+                store(late, third, head + WIDE_HEADS, LATE_HEADS)

@@ -222,12 +222,10 @@ def tile_attention_pa_kernel(
             )
 
         def store(result, third, head, n_heads):
-            for b in range(BATCH):
+            for h in range(n_heads):
                 nc.sync.dma_start(
-                    out=outs[third][b, head : head + n_heads].rearrange(
-                        "h (p j) d -> p h (j d)", j=TOK
-                    ),
-                    in_=result[b:P:BATCH].rearrange("p h j d -> p h (j d)"),
+                    out=outs[third][:, head + h].rearrange("b (p j) d -> p b (j d)", j=TOK),
+                    in_=result[:, h].rearrange("p j d -> p (j d)"),
                 )
 
         cut = WIDE_HEADS * HEAD

@@ -18,6 +18,7 @@ BATCH, TOKENS, DIM = 2, 256, 1536
 HEADS, HEAD = 16, 96
 THIRD = HEADS * HEAD
 HALF = 16
+GROUP = 2 * HALF
 K_PASS = 512
 PASSES = DIM // K_PASS
 TOK = 4
@@ -78,46 +79,41 @@ def load_inputs(nc, keep, x, angles, w_words_in, w_scales_in):
 
 
 def rope_tables(nc, keep, f_sb):
-    by_token = f_sb[:].rearrange("p a (j c) -> p j a c", j=TOK)
-    half_sin = keep.tile([P, TOK, HEAD], F32)
-    nc.scalar.activation(
-        out=half_sin[:].rearrange("p j (a c) -> p j a c", a=3), in_=by_token, func=ACT.Sin, scale=0.5
-    )
-    signed_sin = keep.tile([P, TOK, 3, 2, HALF], F32)
-    halves = by_token.rearrange("p j a (h i) -> p j a h i", h=2)
-    for h in range(2):
+    by_token = f_sb[:].rearrange("p a (j y i) -> p j a y i", j=TOK, y=2)
+    half_sin = keep.tile([P, TOK, 3, 2, HALF], F32)
+    nc.scalar.activation(out=half_sin[:], in_=by_token, func=ACT.Sin, scale=0.5)
+    one_head = keep.tile([P, TOK, 3, 2, 2, HALF], F32)
+    for y in range(2):
         nc.scalar.activation(
-            out=signed_sin[:, :, :, h, :],
-            in_=halves[:, :, :, h, :],
+            out=one_head[:, :, :, y, 1 - y, :],
+            in_=by_token[:, :, :, y, :],
             func=ACT.Sin,
-            scale=(-1.0 if h == 0 else 1.0),
+            scale=(-1.0 if y == 0 else 1.0),
         )
-    squared = keep.tile([P, TOK, HEAD], F32)
+    squared = keep.tile([P, TOK, 3, 2, HALF], F32)
     nc.gpsimd.tensor_tensor(out=squared[:], in0=half_sin[:], in1=half_sin[:], op=ALU.mult)
-    cos_t = keep.tile([P, TOK, PERIODS, HEAD], F32)
-    sin_t = keep.tile([P, TOK, PERIODS, HEAD], F32)
-    one_period = signed_sin[:].rearrange("p j a h i -> p j (a h i)")
-    for j in range(TOK):
+    for y in range(2):
         nc.gpsimd.tensor_scalar(
-            out=cos_t[:, j, :, :],
-            in0=squared[:, j, :].unsqueeze(1).to_broadcast([P, PERIODS, HEAD]),
+            out=one_head[:, :, :, y, y, :],
+            in0=squared[:, :, :, y, :],
             scalar1=-2.0,
             scalar2=1.0,
             op0=ALU.mult,
             op1=ALU.add,
         )
+    table = keep.tile([P, TOK, PERIODS, 2 * HEAD], F32)
+    for j in range(TOK):
         nc.gpsimd.tensor_scalar(
-            out=sin_t[:, j, :, :],
-            in0=one_period[:, j, :].unsqueeze(1).to_broadcast([P, PERIODS, HEAD]),
+            out=table[:, j, :, :],
+            in0=one_head[:, j].rearrange("p a y s i -> p (a y s i)")
+            .unsqueeze(1)
+            .to_broadcast([P, PERIODS, 2 * HEAD]),
             scalar1=1.0,
             scalar2=0.0,
             op0=ALU.mult,
             op1=ALU.add,
         )
-    return (
-        cos_t[:].rearrange("p j r d -> p j (r d)"),
-        sin_t[:].rearrange("p j r d -> p j (r d)"),
-    )
+    return table[:].rearrange("p j r (a c) -> p j (r a) c", c=4 * HALF)
 
 
 def quantise_x(nc, keep, psum, x_sb, ident):
@@ -174,7 +170,7 @@ def tile_attention_pa_kernel(
         x_sb, f_sb, w_words, w_scales = load_inputs(
             nc, keep, x, (f1, f2, f3), Wqkv_words, Wqkv_scales
         )
-        cos_t, sin_t = rope_tables(nc, keep, f_sb)
+        table = rope_tables(nc, keep, f_sb)
         x_codes, x_scales = quantise_x(nc, keep, psum, x_sb, ident)
 
         def project(n, j0, n_tok, c0, cols, n_pass):
@@ -193,31 +189,32 @@ def tile_attention_pa_kernel(
                         )
             return acc
 
-        def products(acc, with_cos, with_sin, j0, n_tok, c0, cols):
+        def products(acc, prod, j0, n_tok, c0, cols):
             toks = slice(j0, j0 + n_tok)
-            here = slice(c0, c0 + cols)
-            window = slice(c0 % HEAD, c0 % HEAD + cols)
+            groups = cols // GROUP
+            first = c0 // GROUP
+            window = (c0 % HEAD) // GROUP
             nc.vector.tensor_tensor(
-                out=with_cos[:, toks, here], in0=acc[:], in1=cos_t[:, toks, window], op=ALU.mult
+                out=prod[:, toks, first : first + groups, :, :],
+                in0=acc[:]
+                .rearrange("p j (g c) -> p j g c", c=GROUP)
+                .unsqueeze(3)
+                .to_broadcast([P, n_tok, groups, 2, GROUP]),
+                in1=table[:, toks, window : window + groups, :].rearrange(
+                    "p j g (y c) -> p j g y c", y=2
+                ),
+                op=ALU.mult,
             )
-            split = "p j (m h i) -> p j m h i"
-            acc_h = acc[:].rearrange(split, h=2, i=HALF)
-            sin_h = sin_t[:, toks, window].rearrange(split, h=2, i=HALF)
-            out_h = with_sin[:, toks, here].rearrange(split, h=2, i=HALF)
-            for h in range(2):
-                nc.vector.tensor_tensor(
-                    out=out_h[:, :, :, h, :],
-                    in0=acc_h[:, :, :, 1 - h, :],
-                    in1=sin_h[:, :, :, h, :],
-                    op=ALU.mult,
-                )
 
-        def add_products(result, with_cos, with_sin, c0, cols):
-            by_head = "p j (h d) -> p j h d"
+        def add_products(result, prod, c0, cols):
+            first = c0 // GROUP
+            halves = prod[:, :, first : first + cols // GROUP, :, :].rearrange(
+                "p j (h a) y (s i) -> p j h (a y) s i", a=3, s=2
+            )
             nc.gpsimd.tensor_tensor(
-                out=result[:].rearrange("p h j d -> p j h d"),
-                in0=with_cos[:, :, c0 : c0 + cols].rearrange(by_head, d=HEAD),
-                in1=with_sin[:, :, c0 : c0 + cols].rearrange(by_head, d=HEAD),
+                out=result[:].rearrange("p h j (a i) -> p j h a i", i=HALF),
+                in0=halves[:, :, :, :, 0, :],
+                in1=halves[:, :, :, :, 1, :],
                 op=ALU.add,
             )
 
@@ -238,12 +235,11 @@ def tile_attention_pa_kernel(
                 early = results.tile([P, WIDE_HEADS, TOK, HEAD], F32, tag="early")
                 late = results.tile([P, LATE_HEADS, TOK, HEAD], F32, tag="late")
                 if rope:
-                    with_cos = scratch.tile([P, TOK, UNIT], F32, tag="with_cos")
-                    with_sin = scratch.tile([P, TOK, UNIT], F32, tag="with_sin")
+                    prod = scratch.tile([P, TOK, UNIT // GROUP, 2, GROUP], F32, tag="prod")
                 for j in range(TOK):
                     acc = project(n, j, 1, 0, WIDE, WIDE)
                     if rope:
-                        products(acc, with_cos, with_sin, j, 1, 0, WIDE)
+                        products(acc, prod, j, 1, 0, WIDE)
                     else:
                         nc.scalar.copy(
                             out=early[:, :, j, :],
@@ -251,12 +247,12 @@ def tile_attention_pa_kernel(
                         )
                         nc.scalar.copy(out=late[:, 0, j, 0:over], in_=acc[:, 0, cut:WIDE])
                 if rope:
-                    add_products(early, with_cos, with_sin, 0, cut)
+                    add_products(early, prod, 0, cut)
                 store(early, third, head, WIDE_HEADS)
                 for j in range(0, TOK, 2):
                     acc = project(n, j, 2, WIDE, NARROW, 128)
                     if rope:
-                        products(acc, with_cos, with_sin, j, 2, WIDE, NARROW)
+                        products(acc, prod, j, 2, WIDE, NARROW)
                     else:
                         nc.scalar.copy(
                             out=late[:, 0, j : j + 2, over:HEAD], in_=acc[:, :, 0 : HEAD - over]
@@ -268,5 +264,5 @@ def tile_attention_pa_kernel(
                             ),
                         )
                 if rope:
-                    add_products(late, with_cos, with_sin, cut, UNIT - cut)
+                    add_products(late, prod, cut, UNIT - cut)
                 store(late, third, head + WIDE_HEADS, LATE_HEADS)

@@ -1,3 +1,4 @@
+import math
 from contextlib import ExitStack
 
 import concourse.mybir as mybir
@@ -24,82 +25,78 @@ PASSES = DIM // K_PASS
 TOK = 4
 PAIRS = TOKENS // TOK
 
-UNIT_HEADS = 8
-UNIT = UNIT_HEADS * HEAD
-WIDE = 512
-NARROW = UNIT - WIDE
-WIDE_HEADS = WIDE // HEAD
-LATE_HEADS = UNIT_HEADS - WIDE_HEADS
+BANK = 512
+BANK_GROUPS = BANK // GROUP
+THIRD_BANKS = THIRD // BANK
 PERIODS = 6
+UNITS = ((0, 0), (1, 0), (0, 1), (2, 0), (1, 1), (0, 2), (2, 1), (1, 2), (2, 2))
 
 FLOPS = 2 * BATCH * TOKENS * DIM * 3 * THIRD
 
 
-def load_inputs(nc, keep, x, angles, w_words_in, w_scales_in):
-    w_scales = keep.tile([P, PASSES, 3 * THIRD], U8, align_bytes=64)
-    nc.vector.memset(w_scales[:].bitcast(I32), 0)
+def load_inputs(nc, keep, head, x, angles, w_words_in, w_scales_in):
+    w_scales = {}
+    for third, bank in UNITS:
+        c = third * THIRD + bank * BANK
+        w_scales[c] = keep.tile([P, PASSES, BANK], U8, align_bytes=64, name="w_scales%d" % c)
+        nc.vector.memset(w_scales[c][:].bitcast(I32), 0)
 
-    f_sb = keep.tile([P, 3, TOK * 2 * HALF], BF16)
+    f_sb = head.tile([P, 3, TOK * GROUP], BF16)
     for a in range(3):
         nc.sync.dma_start(
             out=f_sb[:, a, :],
             in_=angles[a]
             .rearrange("(p j) c -> p (j c)", j=TOK)
             .unsqueeze(1)
-            .to_broadcast([PAIRS, BATCH, TOK * 2 * HALF]),
+            .to_broadcast([PAIRS, BATCH, TOK * GROUP]),
         )
 
     by_partition = x.rearrange("b (p j) k -> p b (j k)", j=TOK)
     x_sb = []
-    for j in range(0, TOK, 2):
-        two_tokens = keep.tile([P, 2, DIM], BF16, name="x_sb%d" % j)
-        nc.scalar.dma_start(
-            out=two_tokens[:].rearrange("p j k -> p (j k)"),
-            in_=by_partition[:, :, j * DIM : (j + 2) * DIM],
-        )
-        x_sb.append(two_tokens)
+    for j in range(TOK):
+        one_token = head.tile([P, DIM], BF16, name="x_sb%d" % j)
+        nc.sync.dma_start(out=one_token[:], in_=by_partition[:, :, j * DIM : (j + 1) * DIM])
+        x_sb.append(one_token)
 
     words_i32 = w_words_in.bitcast(I32).rearrange("g p n -> p g n")
     scales_i32 = w_scales_in.bitcast(I32).rearrange("g q n -> q g n")
     w_words = {}
-    for half in range(2):
-        for third in range(3):
-            n = 2 * third + half
-            w_words[n] = keep.tile([P, PASSES, 2 * UNIT], U8, align_bytes=64, name="w_words%d" % n)
+    for third, bank in UNITS:
+        c = third * THIRD + bank * BANK
+        w_words[c] = keep.tile([P, PASSES, 2 * BANK], U8, align_bytes=64, name="w_words%d" % c)
+        nc.sync.dma_start(
+            out=w_words[c][:].bitcast(I32), in_=words_i32[:, :, c // 2 : (c + BANK) // 2]
+        )
+        for r in range(4):
             nc.sync.dma_start(
-                out=w_words[n][:].bitcast(I32),
-                in_=words_i32[:, :, n * UNIT // 2 : (n + 1) * UNIT // 2],
+                out=w_scales[c][:].bitcast(I32)[r:P:32, :, :],
+                in_=scales_i32[r:16:4, :, c // 4 : (c + BANK) // 4],
             )
-            if n == 0:
-                for r in range(4):
-                    nc.sync.dma_start(
-                        out=w_scales[:].bitcast(I32)[r:P:32, :, :], in_=scales_i32[r:16:4, :, :]
-                    )
     return x_sb, f_sb, w_words, w_scales
 
 
-def rope_tables(nc, keep, f_sb):
+def load_sine_table(nc, head):
+    zeros = head.tile([P, 1], F32)
+    nc.gpsimd.memset(zeros[:], 0.0)
+    unused = head.tile([P, 1], F32)
+    nc.scalar.activation(out=unused[:], in_=zeros[:], func=ACT.Sin)
+
+
+def rope_tables(nc, keep, head, f_sb):
     by_token = f_sb[:].rearrange("p a (j y i) -> p j a y i", j=TOK, y=2)
-    half_sin = keep.tile([P, TOK, 3, 2, HALF], F32)
-    nc.scalar.activation(out=half_sin[:], in_=by_token, func=ACT.Sin, scale=0.5)
-    one_head = keep.tile([P, TOK, 3, 2, 2, HALF], F32)
+    one_head = head.tile([P, TOK, 3, 2, 2, HALF], F32)
     for y in range(2):
+        nc.scalar.activation(
+            out=one_head[:, :, :, y, y, :],
+            in_=by_token[:, :, :, y, :],
+            func=ACT.Sin,
+            bias=math.pi / 2,
+        )
         nc.scalar.activation(
             out=one_head[:, :, :, y, 1 - y, :],
             in_=by_token[:, :, :, y, :],
             func=ACT.Sin,
             scale=(-1.0 if y == 0 else 1.0),
-        )
-    squared = keep.tile([P, TOK, 3, 2, HALF], F32)
-    nc.gpsimd.tensor_tensor(out=squared[:], in0=half_sin[:], in1=half_sin[:], op=ALU.mult)
-    for y in range(2):
-        nc.gpsimd.tensor_scalar(
-            out=one_head[:, :, :, y, y, :],
-            in0=squared[:, :, :, y, :],
-            scalar1=-2.0,
-            scalar2=1.0,
-            op0=ALU.mult,
-            op1=ALU.add,
         )
     table = keep.tile([P, TOK, PERIODS, 2 * HEAD], F32)
     for j in range(TOK):
@@ -113,12 +110,12 @@ def rope_tables(nc, keep, f_sb):
             op0=ALU.mult,
             op1=ALU.add,
         )
-    return table[:].rearrange("p j r (a c) -> p j (r a) c", c=4 * HALF)
+    return table[:].rearrange("p j r (a c) -> p j (r a) c", c=2 * GROUP)
 
 
-def quantise_x(nc, keep, psum, x_sb, ident):
+def quantise_x(nc, keep, head, psum, x_sb, ident):
     tiles = TOK * PASSES
-    grouped = keep.tile([P, tiles, 4 * P], BF16, align_bytes=64)
+    grouped = head.tile([P, tiles, 4 * P], BF16, align_bytes=64)
     x_codes = keep.tile([P, tiles, P], U32, align_bytes=64)
     x_scales = keep.tile([P, tiles, P], U8, align_bytes=64)
 
@@ -133,7 +130,7 @@ def quantise_x(nc, keep, psum, x_sb, ident):
         flipped = psum.tile([P, 4, P], F32, tag="bank")
         for a in range(2):
             j, g = divmod(m + a, PASSES)
-            words = x_sb[j // 2][:, j % 2, :].bitcast(F32)
+            words = x_sb[j][:].bitcast(F32)
             for u in range(2):
                 nc.tensor.transpose(
                     flipped[:, 2 * a + u, :],
@@ -159,110 +156,110 @@ def tile_attention_pa_kernel(
     outs = (out_0, out_1, out_2)
     with ExitStack() as ctx:
         keep = ctx.enter_context(tc.tile_pool(name="keep", bufs=1))
-        scratch = ctx.enter_context(tc.tile_pool(name="scratch", bufs=2))
-        results = ctx.enter_context(tc.tile_pool(name="results", bufs=3))
         psum = ctx.enter_context(tc.psum_pool(name="psum", bufs=8))
 
         ctx.enter_context(tc.manual_schedule())
 
-        ident = keep.tile([P, P], F32)
-        make_identity(nc, ident[:])
-        x_sb, f_sb, w_words, w_scales = load_inputs(
-            nc, keep, x, (f1, f2, f3), Wqkv_words, Wqkv_scales
-        )
-        table = rope_tables(nc, keep, f_sb)
-        x_codes, x_scales = quantise_x(nc, keep, psum, x_sb, ident)
+        prods = {}
+        for third in range(2):
+            prods[third] = keep.tile(
+                [P, TOK, THIRD // GROUP, 2, GROUP], F32, name="prod%d" % third
+            )
+        v_sb = keep.tile([P, HEADS, TOK, HEAD], F32)
 
-        def project(n, j0, n_tok, c0, cols, n_pass):
-            acc = psum.tile([P, n_tok, cols], F32, tag="bank")
-            for t in range(n_tok):
-                for c in range(c0, c0 + cols, n_pass):
-                    for g in range(PASSES):
-                        nc.tensor.matmul_mx(
-                            out=acc[:, t, c - c0 : c - c0 + n_pass],
-                            lhsT=x_codes[:, PASSES * (j0 + t) + g, :].bitcast(FP8X4),
-                            lhsT_scale=x_scales[:, PASSES * (j0 + t) + g, :],
-                            rhs=w_words[n][:, g, 2 * c : 2 * (c + n_pass)].bitcast(FP4X4),
-                            rhs_scale=w_scales[:, g, n * UNIT + c : n * UNIT + c + n_pass],
-                            start=(g == 0),
-                            stop=(g == PASSES - 1),
-                        )
+        with tc.tile_pool(name="head", bufs=1) as head:
+            load_sine_table(nc, head)
+            ident = head.tile([P, P], F32)
+            make_identity(nc, ident[:])
+            x_sb, f_sb, w_words, w_scales = load_inputs(
+                nc, keep, head, x, (f1, f2, f3), Wqkv_words, Wqkv_scales
+            )
+            table = rope_tables(nc, keep, head, f_sb)
+            x_codes, x_scales = quantise_x(nc, keep, head, psum, x_sb, ident)
+
+        results = ctx.enter_context(tc.tile_pool(name="results", bufs=8))
+
+        def project(c, j):
+            acc = psum.tile([P, BANK], F32, tag="bank")
+            for g in range(PASSES):
+                nc.tensor.matmul_mx(
+                    out=acc[:],
+                    lhsT=x_codes[:, PASSES * j + g, :].bitcast(FP8X4),
+                    lhsT_scale=x_scales[:, PASSES * j + g, :],
+                    rhs=w_words[c][:, g, :].bitcast(FP4X4),
+                    rhs_scale=w_scales[c][:, g, :],
+                    start=(g == 0),
+                    stop=(g == PASSES - 1),
+                )
             return acc
 
-        def products(acc, prod, j0, n_tok, c0, cols):
-            toks = slice(j0, j0 + n_tok)
-            groups = cols // GROUP
-            first = c0 // GROUP
-            window = (c0 % HEAD) // GROUP
+        def products(acc, prod, j, bank):
+            first = bank * BANK_GROUPS
+            window = first % 3
             nc.vector.tensor_tensor(
-                out=prod[:, toks, first : first + groups, :, :],
+                out=prod[:, j, first : first + BANK_GROUPS, :, :],
                 in0=acc[:]
-                .rearrange("p j (g c) -> p j g c", c=GROUP)
-                .unsqueeze(3)
-                .to_broadcast([P, n_tok, groups, 2, GROUP]),
-                in1=table[:, toks, window : window + groups, :].rearrange(
-                    "p j g (y c) -> p j g y c", y=2
+                .rearrange("p (g c) -> p g c", c=GROUP)
+                .unsqueeze(2)
+                .to_broadcast([P, BANK_GROUPS, 2, GROUP]),
+                in1=table[:, j, window : window + BANK_GROUPS, :].rearrange(
+                    "p g (y c) -> p g y c", y=2
                 ),
                 op=ALU.mult,
             )
 
-        def add_products(result, prod, c0, cols):
-            first = c0 // GROUP
-            halves = prod[:, :, first : first + cols // GROUP, :, :].rearrange(
+        def add_products(engine, prod, h0, h1):
+            result = results.tile([P, h1 - h0, TOK, HEAD], F32, tag="result")
+            halves = prod[:, :, 3 * h0 : 3 * h1, :, :].rearrange(
                 "p j (h a) y (s i) -> p j h (a y) s i", a=3, s=2
             )
-            nc.gpsimd.tensor_tensor(
+            engine.tensor_tensor(
                 out=result[:].rearrange("p h j (a i) -> p j h a i", i=HALF),
                 in0=halves[:, :, :, :, 0, :],
                 in1=halves[:, :, :, :, 1, :],
                 op=ALU.add,
             )
+            return result
 
-        def store(result, third, head, n_heads):
-            for h in range(n_heads):
-                nc.sync.dma_start(
-                    out=outs[third][:, head + h].rearrange("b (p j) d -> p b (j d)", j=TOK),
-                    in_=result[:, h].rearrange("p j d -> p (j d)"),
-                )
+        def store(queue, rows, third, h):
+            queue.dma_start(
+                out=outs[third][:, h].rearrange("b (p j) d -> p b (j d)", j=TOK),
+                in_=rows.rearrange("p j d -> p (j d)"),
+            )
 
-        cut = WIDE_HEADS * HEAD
-        over = WIDE - cut
-        for half in range(2):
-            for third in range(3):
-                n = 2 * third + half
-                head = half * UNIT_HEADS
-                rope = third < 2
-                early = results.tile([P, WIDE_HEADS, TOK, HEAD], F32, tag="early")
-                late = results.tile([P, LATE_HEADS, TOK, HEAD], F32, tag="late")
-                if rope:
-                    prod = scratch.tile([P, TOK, UNIT // GROUP, 2, GROUP], F32, tag="prod")
-                for j in range(TOK):
-                    acc = project(n, j, 1, 0, WIDE, WIDE)
-                    if rope:
-                        products(acc, prod, j, 1, 0, WIDE)
-                    else:
-                        nc.scalar.copy(
-                            out=early[:, :, j, :],
-                            in_=acc[:, 0, 0:cut].rearrange("p (h d) -> p h d", d=HEAD),
-                        )
-                        nc.scalar.copy(out=late[:, 0, j, 0:over], in_=acc[:, 0, cut:WIDE])
-                if rope:
-                    add_products(early, prod, 0, cut)
-                store(early, third, head, WIDE_HEADS)
-                for j in range(0, TOK, 2):
-                    acc = project(n, j, 2, WIDE, NARROW, 128)
-                    if rope:
-                        products(acc, prod, j, 2, WIDE, NARROW)
-                    else:
-                        nc.scalar.copy(
-                            out=late[:, 0, j : j + 2, over:HEAD], in_=acc[:, :, 0 : HEAD - over]
-                        )
-                        nc.scalar.copy(
-                            out=late[:, 1:LATE_HEADS, j : j + 2, :].rearrange("p h j d -> p j h d"),
-                            in_=acc[:, :, HEAD - over : NARROW].rearrange(
-                                "p j (h d) -> p j h d", d=HEAD
-                            ),
-                        )
-                if rope:
-                    add_products(late, prod, cut, UNIT - cut)
-                store(late, third, head + WIDE_HEADS, LATE_HEADS)
+        last_sums = []
+        for third, bank in UNITS:
+            c0 = bank * BANK
+            h0, h1 = c0 // HEAD, (c0 + BANK) // HEAD
+            last = bank == THIRD_BANKS - 1
+            for j in range(TOK):
+                acc = project(third * THIRD + c0, j)
+                if third < 2:
+                    products(acc, prods[third], j, bank)
+                else:
+                    lead = (HEAD - c0 % HEAD) % HEAD
+                    whole = (BANK - lead) // HEAD
+                    rest = BANK - lead - whole * HEAD
+                    ha = (c0 + lead) // HEAD
+                    if lead:
+                        nc.scalar.copy(out=v_sb[:, ha - 1, j, HEAD - lead :], in_=acc[:, 0:lead])
+                    nc.scalar.copy(
+                        out=v_sb[:, ha : ha + whole, j, :],
+                        in_=acc[:, lead : lead + whole * HEAD].rearrange("p (h d) -> p h d", d=HEAD),
+                    )
+                    if rest:
+                        nc.scalar.copy(out=v_sb[:, ha + whole, j, 0:rest], in_=acc[:, BANK - rest :])
+            if third == 2:
+                for h in range(h0, h1):
+                    store(nc.scalar, v_sb[:, h], third, h)
+            elif third == 1 and last:
+                for h in range(h0, h1, 2):
+                    last_sums.append((h, add_products(nc.vector, prods[third], h, h + 2)))
+            else:
+                for h in range(h0, h1, 3):
+                    result = add_products(nc.gpsimd, prods[third], h, min(h + 3, h1))
+                    for k in range(h, min(h + 3, h1)):
+                        store(nc.sync, result[:, k - h], third, k)
+        for h, result in last_sums:
+            for k in range(2):
+                store(nc.scalar, result[:, k], 1, h + k)

@@ -31,6 +31,9 @@ THIRD_BANKS = THIRD // BANK
 PERIODS = 6
 UNITS = ((0, 0), (1, 0), (0, 1), (2, 0), (1, 1), (0, 2), (2, 1), (1, 2), (2, 2))
 
+WARM_UP = 8
+STAY_WARM = 3
+
 FLOPS = 2 * BATCH * TOKENS * DIM * 3 * THIRD
 
 
@@ -113,7 +116,13 @@ def rope_tables(nc, keep, head, f_sb):
     return table[:].rearrange("p j r (a c) -> p j (r a) c", c=2 * GROUP)
 
 
-def quantise_x(nc, keep, head, psum, x_sb, ident):
+def keep_busy(nc, psum, zeros, n):
+    unread = psum.tile([P, BANK], F32, tag="bank")
+    for i in range(n):
+        nc.tensor.matmul(out=unread[:], lhsT=zeros[:, 0:P], rhs=zeros[:], start=True, stop=True)
+
+
+def quantise_x(nc, keep, head, psum, x_sb, ident, zeros):
     tiles = TOK * PASSES
     grouped = head.tile([P, tiles, 4 * P], BF16, align_bytes=64)
     x_codes = keep.tile([P, tiles, P], U32, align_bytes=64)
@@ -126,7 +135,10 @@ def quantise_x(nc, keep, head, psum, x_sb, ident):
             in_=grouped[:, m : m + 2, :].rearrange("p a c -> p (a c)"),
         )
 
+    keep_busy(nc, psum, zeros, WARM_UP)
     for m in range(0, tiles, 2):
+        if m == tiles // 2:
+            keep_busy(nc, psum, zeros, STAY_WARM)
         flipped = psum.tile([P, 4, P], F32, tag="bank")
         for a in range(2):
             j, g = divmod(m + a, PASSES)
@@ -168,6 +180,8 @@ def tile_attention_pa_kernel(
         v_sb = keep.tile([P, HEADS, TOK, HEAD], F32)
 
         with tc.tile_pool(name="head", bufs=1) as head:
+            idle_operand = head.tile([P, BANK], BF16)
+            nc.vector.memset(idle_operand[:], 0.0)
             load_sine_table(nc, head)
             ident = head.tile([P, P], F32)
             make_identity(nc, ident[:])
@@ -175,7 +189,9 @@ def tile_attention_pa_kernel(
                 nc, keep, head, x, (f1, f2, f3), Wqkv_words, Wqkv_scales
             )
             table = rope_tables(nc, keep, head, f_sb)
-            x_codes, x_scales = quantise_x(nc, keep, head, psum, x_sb, ident)
+            x_codes, x_scales = quantise_x(
+                nc, keep, head, psum, x_sb, ident, idle_operand
+            )
 
         results = ctx.enter_context(tc.tile_pool(name="results", bufs=8))
 

@@ -27,9 +27,10 @@ PAIRS = TOKENS // TOK
 
 BANK = 512
 BANK_GROUPS = BANK // GROUP
+NARROW = 128
 THIRD_BANKS = THIRD // BANK
 PERIODS = 6
-UNITS = ((0, 0), (1, 0), (0, 1), (2, 0), (1, 1), (0, 2), (2, 1), (1, 2), (2, 2))
+UNITS = ((2, 0), (0, 0), (1, 0), (2, 1), (0, 1), (1, 1), (2, 2), (0, 2), (1, 2))
 
 WARM_UP = 8
 STAY_WARM = 3
@@ -193,7 +194,7 @@ def tile_attention_pa_kernel(
                 nc, keep, head, psum, x_sb, ident, idle_operand
             )
 
-        results = ctx.enter_context(tc.tile_pool(name="results", bufs=8))
+        results = ctx.enter_context(tc.tile_pool(name="results", bufs=4))
 
         def project(c, j):
             acc = psum.tile([P, BANK], F32, tag="bank")
@@ -224,18 +225,32 @@ def tile_attention_pa_kernel(
                 op=ALU.mult,
             )
 
-        def add_products(engine, prod, h0, h1):
-            result = results.tile([P, h1 - h0, TOK, HEAD], F32, tag="result")
-            halves = prod[:, :, 3 * h0 : 3 * h1, :, :].rearrange(
+        def project_narrow(c, n):
+            acc = psum.tile([P, TOK, NARROW], F32, tag="bank")
+            for j in range(TOK):
+                for g in range(PASSES):
+                    nc.tensor.matmul_mx(
+                        out=acc[:, j, :],
+                        lhsT=x_codes[:, PASSES * j + g, :].bitcast(FP8X4),
+                        lhsT_scale=x_scales[:, PASSES * j + g, :],
+                        rhs=w_words[c][:, g, 2 * NARROW * n : 2 * NARROW * (n + 1)].bitcast(FP4X4),
+                        rhs_scale=w_scales[c][:, g, NARROW * n : NARROW * (n + 1)],
+                        start=(g == 0),
+                        stop=(g == PASSES - 1),
+                    )
+            return acc
+
+        def add_products(engine, prod, result, h0, j0, j1):
+            h1 = h0 + result.shape[1]
+            halves = prod[:, j0:j1, 3 * h0 : 3 * h1, :, :].rearrange(
                 "p j (h a) y (s i) -> p j h (a y) s i", a=3, s=2
             )
             engine.tensor_tensor(
-                out=result[:].rearrange("p h j (a i) -> p j h a i", i=HALF),
+                out=result[:, :, j0:j1, :].rearrange("p h j (a i) -> p j h a i", i=HALF),
                 in0=halves[:, :, :, :, 0, :],
                 in1=halves[:, :, :, :, 1, :],
                 op=ALU.add,
             )
-            return result
 
         def store(queue, rows, third, h):
             queue.dma_start(
@@ -243,39 +258,54 @@ def tile_attention_pa_kernel(
                 in_=rows.rearrange("p j d -> p (j d)"),
             )
 
-        last_sums = []
+        def copy_v(acc, c0, j):
+            lead = (HEAD - c0 % HEAD) % HEAD
+            whole = (BANK - lead) // HEAD
+            rest = BANK - lead - whole * HEAD
+            ha = (c0 + lead) // HEAD
+            if lead:
+                nc.scalar.copy(out=v_sb[:, ha - 1, j, HEAD - lead :], in_=acc[:, 0:lead])
+            nc.scalar.copy(
+                out=v_sb[:, ha : ha + whole, j, :],
+                in_=acc[:, lead : lead + whole * HEAD].rearrange("p (h d) -> p h d", d=HEAD),
+            )
+            if rest:
+                nc.scalar.copy(out=v_sb[:, ha + whole, j, 0:rest], in_=acc[:, BANK - rest :])
+
         for third, bank in UNITS:
             c0 = bank * BANK
             h0, h1 = c0 // HEAD, (c0 + BANK) // HEAD
             last = bank == THIRD_BANKS - 1
-            for j in range(TOK):
-                acc = project(third * THIRD + c0, j)
-                if third < 2:
-                    products(acc, prods[third], j, bank)
-                else:
-                    lead = (HEAD - c0 % HEAD) % HEAD
-                    whole = (BANK - lead) // HEAD
-                    rest = BANK - lead - whole * HEAD
-                    ha = (c0 + lead) // HEAD
-                    if lead:
-                        nc.scalar.copy(out=v_sb[:, ha - 1, j, HEAD - lead :], in_=acc[:, 0:lead])
-                    nc.scalar.copy(
-                        out=v_sb[:, ha : ha + whole, j, :],
-                        in_=acc[:, lead : lead + whole * HEAD].rearrange("p (h d) -> p h d", d=HEAD),
-                    )
-                    if rest:
-                        nc.scalar.copy(out=v_sb[:, ha + whole, j, 0:rest], in_=acc[:, BANK - rest :])
-            if third == 2:
+            if third == 2 and last:
+                for n in range(BANK // NARROW):
+                    acc = project_narrow(third * THIRD + c0, n)
+                    lo, hi = c0 + n * NARROW, c0 + (n + 1) * NARROW
+                    for h in range(lo // HEAD, (hi - 1) // HEAD + 1):
+                        a, b = max(lo, h * HEAD), min(hi, (h + 1) * HEAD)
+                        nc.scalar.copy(
+                            out=v_sb[:, h, :, a - h * HEAD : b - h * HEAD],
+                            in_=acc[:, :, a - lo : b - lo],
+                        )
+                    for h in range(max(h0, lo // HEAD), hi // HEAD):
+                        store(nc.scalar, v_sb[:, h], third, h)
+            elif third == 2:
+                for j in range(TOK):
+                    copy_v(project(third * THIRD + c0, j), c0, j)
                 for h in range(h0, h1):
                     store(nc.scalar, v_sb[:, h], third, h)
             elif third == 1 and last:
+                for j in range(TOK):
+                    products(project(third * THIRD + c0, j), prods[third], j, bank)
                 for h in range(h0, h1, 2):
-                    last_sums.append((h, add_products(nc.vector, prods[third], h, h + 2)))
+                    result = results.tile([P, 2, TOK, HEAD], F32, tag="last", bufs=3)
+                    add_products(nc.vector, prods[third], result, h, 0, TOK)
+                    for k in range(2):
+                        store(nc.sync, result[:, k], third, h + k)
             else:
-                for h in range(h0, h1, 3):
-                    result = add_products(nc.gpsimd, prods[third], h, min(h + 3, h1))
-                    for k in range(h, min(h + 3, h1)):
-                        store(nc.sync, result[:, k - h], third, k)
-        for h, result in last_sums:
-            for k in range(2):
-                store(nc.scalar, result[:, k], 1, h + k)
+                result = results.tile([P, h1 - h0, TOK, HEAD], F32, tag="result")
+                for j in range(TOK):
+                    products(project(third * THIRD + c0, j), prods[third], j, bank)
+                    if j % 2 == 1:
+                        add_products(nc.gpsimd, prods[third], result, h0, j - 1, j + 1)
+                for h in range(h0, h1):
+                    store(nc.sync, result[:, h - h0], third, h)

@@ -102,17 +102,17 @@ def rope_tables(nc, keep, head, f_sb):
             func=ACT.Sin,
             scale=(-1.0 if y == 0 else 1.0),
         )
+    return one_head
+
+
+def spread_factors(nc, keep, one_head):
     table = keep.tile([P, TOK, PERIODS, 2 * HEAD], F32)
     for j in range(TOK):
-        nc.gpsimd.tensor_scalar(
+        nc.vector.tensor_copy(
             out=table[:, j, :, :],
-            in0=one_head[:, j].rearrange("p a y s i -> p (a y s i)")
+            in_=one_head[:, j].rearrange("p a y s i -> p (a y s i)")
             .unsqueeze(1)
             .to_broadcast([P, PERIODS, 2 * HEAD]),
-            scalar1=1.0,
-            scalar2=0.0,
-            op0=ALU.mult,
-            op1=ALU.add,
         )
     return table[:].rearrange("p j r (a c) -> p j (r a) c", c=2 * GROUP)
 
@@ -189,10 +189,11 @@ def tile_attention_pa_kernel(
             x_sb, f_sb, w_words, w_scales = load_inputs(
                 nc, keep, head, x, (f1, f2, f3), Wqkv_words, Wqkv_scales
             )
-            table = rope_tables(nc, keep, head, f_sb)
+            one_head = rope_tables(nc, keep, head, f_sb)
             x_codes, x_scales = quantise_x(
                 nc, keep, head, psum, x_sb, ident, idle_operand
             )
+            table = spread_factors(nc, keep, one_head)
 
         results = ctx.enter_context(tc.tile_pool(name="results", bufs=4))
 

@@ -306,7 +306,10 @@ def tile_attention_pa_kernel(
                 result = results.tile([P, h1 - h0, TOK, HEAD], F32, tag="result")
                 for j in range(TOK):
                     products(project(third * THIRD + c0, j), prods[third], j, bank)
-                    if j % 2 == 1:
-                        add_products(nc.gpsimd, prods[third], result, h0, j - 1, j + 1)
-                for h in range(h0, h1):
-                    store(nc.sync, result[:, h - h0], third, h)
+                    if j == 1:
+                        add_products(nc.gpsimd, prods[third], result, h0, 0, 2)
+                for h in range(h0, h1, 3):
+                    n = min(3, h1 - h)
+                    add_products(nc.gpsimd, prods[third], result[:, h - h0 : h - h0 + n], h, 2, TOK)
+                    for k in range(h, h + n):
+                        store(nc.sync, result[:, k - h0], third, k)

@@ -27,7 +27,6 @@ PAIRS = TOKENS // TOK
 
 BANK = 512
 BANK_GROUPS = BANK // GROUP
-NARROW = 128
 THIRD_BANKS = THIRD // BANK
 PERIODS = 6
 UNITS = ((2, 0), (0, 0), (1, 0), (2, 1), (0, 1), (1, 1), (2, 2), (0, 2), (1, 2))
@@ -226,21 +225,6 @@ def tile_attention_pa_kernel(
                 op=ALU.mult,
             )
 
-        def project_narrow(c, n):
-            acc = psum.tile([P, TOK, NARROW], F32, tag="bank")
-            for j in range(TOK):
-                for g in range(PASSES):
-                    nc.tensor.matmul_mx(
-                        out=acc[:, j, :],
-                        lhsT=x_codes[:, PASSES * j + g, :].bitcast(FP8X4),
-                        lhsT_scale=x_scales[:, PASSES * j + g, :],
-                        rhs=w_words[c][:, g, 2 * NARROW * n : 2 * NARROW * (n + 1)].bitcast(FP4X4),
-                        rhs_scale=w_scales[c][:, g, NARROW * n : NARROW * (n + 1)],
-                        start=(g == 0),
-                        stop=(g == PASSES - 1),
-                    )
-            return acc
-
         def add_products(engine, prod, result, h0, j0, j1):
             h1 = h0 + result.shape[1]
             halves = prod[:, j0:j1, 3 * h0 : 3 * h1, :, :].rearrange(
@@ -277,19 +261,7 @@ def tile_attention_pa_kernel(
             c0 = bank * BANK
             h0, h1 = c0 // HEAD, (c0 + BANK) // HEAD
             last = bank == THIRD_BANKS - 1
-            if third == 2 and last:
-                for n in range(BANK // NARROW):
-                    acc = project_narrow(third * THIRD + c0, n)
-                    lo, hi = c0 + n * NARROW, c0 + (n + 1) * NARROW
-                    for h in range(lo // HEAD, (hi - 1) // HEAD + 1):
-                        a, b = max(lo, h * HEAD), min(hi, (h + 1) * HEAD)
-                        nc.scalar.copy(
-                            out=v_sb[:, h, :, a - h * HEAD : b - h * HEAD],
-                            in_=acc[:, :, a - lo : b - lo],
-                        )
-                    for h in range(max(h0, lo // HEAD), hi // HEAD):
-                        store(nc.scalar, v_sb[:, h], third, h)
-            elif third == 2:
+            if third == 2:
                 for j in range(TOK):
                     copy_v(project(third * THIRD + c0, j), c0, j)
                 for h in range(h0, h1):

@@ -29,18 +29,28 @@ BANK = 512
 BANK_GROUPS = BANK // GROUP
 THIRD_BANKS = THIRD // BANK
 PERIODS = 6
-UNITS = ((2, 0), (0, 0), (1, 0), (2, 1), (0, 1), (1, 1), (2, 2), (0, 2), (1, 2))
-
 WARM_UP = 8
 STAY_WARM = 3
 
 FLOPS = 2 * BATCH * TOKENS * DIM * 3 * THIRD
 
 
-def load_inputs(nc, keep, head, x, angles, w_words_in, w_scales_in):
+def bank_order():
+    rope = [(third, bank, j) for bank in range(THIRD_BANKS) for third in range(2) for j in range(TOK)]
+    v = [(2, bank, j) for bank in range(THIRD_BANKS) for j in range(TOK)]
+    order = v[:TOK]
+    for i in range(0, len(rope), 3):
+        order = order + v[TOK + i // 3 : TOK + i // 3 + 1] + rope[i : i + 3]
+    return order
+
+
+def load_inputs(nc, keep, head, x, angles, w_words_in, w_scales_in, order):
+    loads = []
+    for third, bank, j in order:
+        if third * THIRD + bank * BANK not in loads:
+            loads.append(third * THIRD + bank * BANK)
     w_scales = {}
-    for third, bank in UNITS:
-        c = third * THIRD + bank * BANK
+    for c in loads:
         w_scales[c] = keep.tile([P, PASSES, BANK], U8, align_bytes=64, name="w_scales%d" % c)
         nc.vector.memset(w_scales[c][:].bitcast(I32), 0)
 
@@ -64,8 +74,7 @@ def load_inputs(nc, keep, head, x, angles, w_words_in, w_scales_in):
     words_i32 = w_words_in.bitcast(I32).rearrange("g p n -> p g n")
     scales_i32 = w_scales_in.bitcast(I32).rearrange("g q n -> q g n")
     w_words = {}
-    for third, bank in UNITS:
-        c = third * THIRD + bank * BANK
+    for c in loads:
         w_words[c] = keep.tile([P, PASSES, 2 * BANK], U8, align_bytes=64, name="w_words%d" % c)
         nc.sync.dma_start(
             out=w_words[c][:].bitcast(I32), in_=words_i32[:, :, c // 2 : (c + BANK) // 2]
@@ -179,6 +188,7 @@ def tile_attention_pa_kernel(
             )
         v_sb = keep.tile([P, HEADS, TOK, HEAD], F32)
 
+        order = bank_order()
         with tc.tile_pool(name="head", bufs=1) as head:
             idle_operand = head.tile([P, BANK], BF16)
             nc.vector.memset(idle_operand[:], 0.0)
@@ -186,7 +196,7 @@ def tile_attention_pa_kernel(
             ident = head.tile([P, P], F32)
             make_identity(nc, ident[:])
             x_sb, f_sb, w_words, w_scales = load_inputs(
-                nc, keep, head, x, (f1, f2, f3), Wqkv_words, Wqkv_scales
+                nc, keep, head, x, (f1, f2, f3), Wqkv_words, Wqkv_scales, order
             )
             one_head = rope_tables(nc, keep, head, f_sb)
             x_codes, x_scales = quantise_x(
@@ -257,31 +267,35 @@ def tile_attention_pa_kernel(
             if rest:
                 nc.scalar.copy(out=v_sb[:, ha + whole, j, 0:rest], in_=acc[:, BANK - rest :])
 
-        for third, bank in UNITS:
+        result = None
+        for third, bank, j in order:
             c0 = bank * BANK
             h0, h1 = c0 // HEAD, (c0 + BANK) // HEAD
-            last = bank == THIRD_BANKS - 1
+            acc = project(third * THIRD + c0, j)
             if third == 2:
-                for j in range(TOK):
-                    copy_v(project(third * THIRD + c0, j), c0, j)
-                for h in range(h0, h1):
-                    store(nc.scalar, v_sb[:, h], third, h)
-            elif third == 1 and last:
-                for j in range(TOK):
-                    products(project(third * THIRD + c0, j), prods[third], j, bank)
-                for h in range(h0, h1, 2):
-                    result = results.tile([P, 2, TOK, HEAD], F32, tag="last", bufs=3)
-                    add_products(nc.vector, prods[third], result, h, 0, TOK)
-                    for k in range(2):
-                        store(nc.sync, result[:, k], third, h + k)
+                copy_v(acc, c0, j)
+                if j == TOK - 1:
+                    for h in range(h0, h1):
+                        store(nc.scalar, v_sb[:, h], third, h)
+            elif (third, bank) == (1, THIRD_BANKS - 1):
+                products(acc, prods[third], j, bank)
+                if j == TOK - 1:
+                    for h in range(h0, h1, 2):
+                        pair = results.tile([P, 2, TOK, HEAD], F32, tag="last", bufs=3)
+                        add_products(nc.vector, prods[third], pair, h, 0, TOK)
+                        for k in range(2):
+                            store(nc.sync, pair[:, k], third, h + k)
             else:
-                result = results.tile([P, h1 - h0, TOK, HEAD], F32, tag="result")
-                for j in range(TOK):
-                    products(project(third * THIRD + c0, j), prods[third], j, bank)
-                    if j == 1:
-                        add_products(nc.gpsimd, prods[third], result, h0, 0, 2)
-                for h in range(h0, h1, 3):
-                    n = min(3, h1 - h)
-                    add_products(nc.gpsimd, prods[third], result[:, h - h0 : h - h0 + n], h, 2, TOK)
-                    for k in range(h, h + n):
-                        store(nc.sync, result[:, k - h0], third, k)
+                if j == 0:
+                    result = results.tile([P, h1 - h0, TOK, HEAD], F32, tag="result")
+                products(acc, prods[third], j, bank)
+                if j == 1:
+                    add_products(nc.gpsimd, prods[third], result, h0, 0, 2)
+                if j == TOK - 1:
+                    for h in range(h0, h1, 3):
+                        n = min(3, h1 - h)
+                        add_products(
+                            nc.gpsimd, prods[third], result[:, h - h0 : h - h0 + n], h, 2, TOK
+                        )
+                        for k in range(h, h + n):
+                            store(nc.sync, result[:, k - h0], third, k)

@@ -31,6 +31,8 @@ THIRD_BANKS = THIRD // BANK
 PERIODS = 6
 WARM_UP = 8
 STAY_WARM = 3
+LOADS_AHEAD = 9
+STORE_LAG = 5
 
 FLOPS = 2 * BATCH * TOKENS * DIM * 3 * THIRD
 
@@ -38,10 +40,10 @@ FLOPS = 2 * BATCH * TOKENS * DIM * 3 * THIRD
 def bank_order():
     rope = [(third, bank, j) for bank in range(THIRD_BANKS) for third in range(2) for j in range(TOK)]
     v = [(2, bank, j) for bank in range(THIRD_BANKS) for j in range(TOK)]
-    order = v[:TOK]
+    order = v[:1]
     for i in range(0, len(rope), 3):
-        order = order + v[TOK + i // 3 : TOK + i // 3 + 1] + rope[i : i + 3]
-    return order
+        order = order + rope[i : i + 3] + v[1 + i // 3 : 2 + i // 3]
+    return order + v[1 + len(rope) // 3 :]
 
 
 def load_inputs(nc, keep, head, x, angles, w_words_in, w_scales_in, order):
@@ -76,6 +78,8 @@ def load_inputs(nc, keep, head, x, angles, w_words_in, w_scales_in, order):
     w_words = {}
     for c in loads:
         w_words[c] = keep.tile([P, PASSES, 2 * BANK], U8, align_bytes=64, name="w_words%d" % c)
+
+    def load_unit(c):
         nc.sync.dma_start(
             out=w_words[c][:].bitcast(I32), in_=words_i32[:, :, c // 2 : (c + BANK) // 2]
         )
@@ -84,7 +88,10 @@ def load_inputs(nc, keep, head, x, angles, w_words_in, w_scales_in, order):
                 out=w_scales[c][:].bitcast(I32)[r:P:32, :, :],
                 in_=scales_i32[r:16:4, :, c // 4 : (c + BANK) // 4],
             )
-    return x_sb, f_sb, w_words, w_scales
+
+    for c in loads[:LOADS_AHEAD]:
+        load_unit(c)
+    return x_sb, f_sb, w_words, w_scales, loads[LOADS_AHEAD:], load_unit
 
 
 def load_sine_table(nc, head):
@@ -113,16 +120,13 @@ def rope_tables(nc, keep, head, f_sb):
     return one_head
 
 
-def spread_factors(nc, keep, one_head):
-    table = keep.tile([P, TOK, PERIODS, 2 * HEAD], F32)
-    for j in range(TOK):
-        nc.vector.tensor_copy(
-            out=table[:, j, :, :],
-            in_=one_head[:, j].rearrange("p a y s i -> p (a y s i)")
-            .unsqueeze(1)
-            .to_broadcast([P, PERIODS, 2 * HEAD]),
-        )
-    return table[:].rearrange("p j r (a c) -> p j (r a) c", c=2 * GROUP)
+def spread_factors(copy, table, one_head, j):
+    copy(
+        out=table[:, j, :, :],
+        in_=one_head[:, j].rearrange("p a y s i -> p (a y s i)")
+        .unsqueeze(1)
+        .to_broadcast([P, PERIODS, 2 * HEAD]),
+    )
 
 
 def keep_busy(nc, psum, zeros, n):
@@ -131,7 +135,7 @@ def keep_busy(nc, psum, zeros, n):
         nc.tensor.matmul(out=unread[:], lhsT=zeros[:, 0:P], rhs=zeros[:], start=True, stop=True)
 
 
-def quantise_x(nc, keep, head, psum, x_sb, ident, zeros):
+def quantise_x(nc, keep, head, psum, x_sb, ident, zeros, table, one_head):
     tiles = TOK * PASSES
     grouped = head.tile([P, tiles, 4 * P], BF16, align_bytes=64)
     x_codes = keep.tile([P, tiles, P], U32, align_bytes=64)
@@ -160,13 +164,13 @@ def quantise_x(nc, keep, head, psum, x_sb, ident, zeros):
                 )
         side_by_side = grouped[:, m : m + 2, :].bitcast(F32).rearrange("p a (r u) -> p a r u", u=2)
         pairs = flipped[:].rearrange("p (a u) r -> p a r u", u=2)
-        if m % 4 == 0:
-            nc.vector.tensor_copy(out=side_by_side, in_=pairs)
-        else:
-            nc.scalar.copy(out=side_by_side, in_=pairs)
+        nc.scalar.copy(out=side_by_side, in_=pairs)
         if m > 0:
             quantise(m - 2)
+        if m // 2 < TOK - 1:
+            spread_factors(nc.vector.tensor_copy, table, one_head, m // 2)
     quantise(tiles - 2)
+    spread_factors(nc.scalar.copy, table, one_head, TOK - 1)
     return x_codes, x_scales
 
 
@@ -195,14 +199,15 @@ def tile_attention_pa_kernel(
             load_sine_table(nc, head)
             ident = head.tile([P, P], F32)
             make_identity(nc, ident[:])
-            x_sb, f_sb, w_words, w_scales = load_inputs(
+            x_sb, f_sb, w_words, w_scales, later_loads, load_unit = load_inputs(
                 nc, keep, head, x, (f1, f2, f3), Wqkv_words, Wqkv_scales, order
             )
             one_head = rope_tables(nc, keep, head, f_sb)
+            periods = keep.tile([P, TOK, PERIODS, 2 * HEAD], F32)
             x_codes, x_scales = quantise_x(
-                nc, keep, head, psum, x_sb, ident, idle_operand
+                nc, keep, head, psum, x_sb, ident, idle_operand, periods, one_head
             )
-            table = spread_factors(nc, keep, one_head)
+            table = periods[:].rearrange("p j r (a c) -> p j (r a) c", c=2 * GROUP)
 
         results = ctx.enter_context(tc.tile_pool(name="results", bufs=4))
 
@@ -268,7 +273,13 @@ def tile_attention_pa_kernel(
                 nc.scalar.copy(out=v_sb[:, ha + whole, j, 0:rest], in_=acc[:, BANK - rest :])
 
         result = None
-        for third, bank, j in order:
+        waiting = []
+        for step, (third, bank, j) in enumerate(order + [(None, 0, 0)] * (STORE_LAG + 2)):
+            while waiting and waiting[0][0] <= step:
+                store(nc.sync, waiting[0][1], waiting[0][2], waiting[0][3])
+                waiting = waiting[1:]
+            if third is None:
+                continue
             c0 = bank * BANK
             h0, h1 = c0 // HEAD, (c0 + BANK) // HEAD
             acc = project(third * THIRD + c0, j)
@@ -276,7 +287,7 @@ def tile_attention_pa_kernel(
                 copy_v(acc, c0, j)
                 if j == TOK - 1:
                     for h in range(h0, h1):
-                        store(nc.scalar, v_sb[:, h], third, h)
+                        store(nc.sync, v_sb[:, h], third, h)
             elif (third, bank) == (1, THIRD_BANKS - 1):
                 products(acc, prods[third], j, bank)
                 if j == TOK - 1:
@@ -284,7 +295,9 @@ def tile_attention_pa_kernel(
                         pair = results.tile([P, 2, TOK, HEAD], F32, tag="last", bufs=3)
                         add_products(nc.vector, prods[third], pair, h, 0, TOK)
                         for k in range(2):
-                            store(nc.sync, pair[:, k], third, h + k)
+                            waiting.append(
+                                (step + STORE_LAG - 1 + (h - h0) // 2, pair[:, k], third, h + k)
+                            )
             else:
                 if j == 0:
                     result = results.tile([P, h1 - h0, TOK, HEAD], F32, tag="result")
@@ -298,4 +311,4 @@ def tile_attention_pa_kernel(
                             nc.gpsimd, prods[third], result[:, h - h0 : h - h0 + n], h, 2, TOK
                         )
                         for k in range(h, h + n):
-                            store(nc.sync, result[:, k - h0], third, k)
+                            waiting.append((step + STORE_LAG + (h - h0) // 3, result[:, k - h0], third, k))

@@ -305,8 +305,9 @@ def tile_attention_pa_kernel(
                 if j == 1:
                     add_products(nc.gpsimd, prods[third], result, h0, 0, 2)
                 if j == TOK - 1:
-                    for h in range(h0, h1, 3):
-                        n = min(3, h1 - h)
+                    lot = 3 if bank == THIRD_BANKS - 1 else h1 - h0
+                    for h in range(h0, h1, lot):
+                        n = min(lot, h1 - h)
                         add_products(
                             nc.gpsimd, prods[third], result[:, h - h0 : h - h0 + n], h, 2, TOK
                         )

@@ -252,10 +252,12 @@ def tile_attention_pa_kernel(
                 op=ALU.add,
             )
 
-        def store(queue, rows, third, h):
+        def store(queue, rows, third, h, j0=0, j1=TOK):
             queue.dma_start(
-                out=outs[third][:, h].rearrange("b (p j) d -> p b (j d)", j=TOK),
-                in_=rows.rearrange("p j d -> p (j d)"),
+                out=outs[third][:, h].rearrange("b (p j) d -> p b (j d)", j=TOK)[
+                    :, :, j0 * HEAD : j1 * HEAD
+                ],
+                in_=rows[:, j0:j1, :].rearrange("p j d -> p (j d)"),
             )
 
         def copy_v(acc, c0, j):
@@ -285,7 +287,10 @@ def tile_attention_pa_kernel(
             acc = project(third * THIRD + c0, j)
             if third == 2:
                 copy_v(acc, c0, j)
-                if j == TOK - 1:
+                if bank == 1 and j % 2 == 1:
+                    for h in range(h0, h1):
+                        store(nc.sync, v_sb[:, h], third, h, j - 1, j + 1)
+                elif bank != 1 and j == TOK - 1:
                     for h in range(h0, h1):
                         store(nc.sync, v_sb[:, h], third, h)
             elif (third, bank) == (1, THIRD_BANKS - 1):

import math
from contextlib import ExitStack

import concourse.mybir as mybir
from concourse.masks import make_identity

F32 = mybir.dt.float32
BF16 = mybir.dt.bfloat16
I32 = mybir.dt.int32
U32 = mybir.dt.uint32
U8 = mybir.dt.uint8
FP8X4 = mybir.dt.float8_e4m3fn_x4
FP4X4 = mybir.dt.float4_e2m1fn_x4
ACT = mybir.ActivationFunctionType
ALU = mybir.AluOpType

P = 128
BATCH, TOKENS, DIM = 2, 256, 1536
HEADS, HEAD = 16, 96
THIRD = HEADS * HEAD
HALF = 16
GROUP = 2 * HALF
K_PASS = 512
PASSES = DIM // K_PASS
TOK = 4
PAIRS = TOKENS // TOK

BANK = 512
BANK_GROUPS = BANK // GROUP
THIRD_BANKS = THIRD // BANK
PERIODS = 6
WARM_UP = 8
STAY_WARM = 3
LOADS_AHEAD = 9
STORE_LAG = 5

FLOPS = 2 * BATCH * TOKENS * DIM * 3 * THIRD


def bank_order():
    rope = [(third, bank, j) for bank in range(THIRD_BANKS) for third in range(2) for j in range(TOK)]
    v = [(2, bank, j) for bank in range(THIRD_BANKS) for j in range(TOK)]
    order = v[:1]
    for i in range(0, len(rope), 3):
        order = order + rope[i : i + 3] + v[1 + i // 3 : 2 + i // 3]
    return order + v[1 + len(rope) // 3 :]


def load_inputs(nc, keep, head, x, angles, w_words_in, w_scales_in, order):
    loads = []
    for third, bank, j in order:
        if third * THIRD + bank * BANK not in loads:
            loads.append(third * THIRD + bank * BANK)
    w_scales = {}
    for c in loads:
        w_scales[c] = keep.tile([P, PASSES, BANK], U8, align_bytes=64, name="w_scales%d" % c)
        nc.vector.memset(w_scales[c][:].bitcast(I32), 0)

    f_sb = head.tile([P, 3, TOK * GROUP], BF16)
    for a in range(3):
        nc.sync.dma_start(
            out=f_sb[:, a, :],
            in_=angles[a]
            .rearrange("(p j) c -> p (j c)", j=TOK)
            .unsqueeze(1)
            .to_broadcast([PAIRS, BATCH, TOK * GROUP]),
        )

    by_partition = x.rearrange("b (p j) k -> p b (j k)", j=TOK)
    x_sb = []
    for j in range(TOK):
        one_token = head.tile([P, DIM], BF16, name="x_sb%d" % j)
        nc.sync.dma_start(out=one_token[:], in_=by_partition[:, :, j * DIM : (j + 1) * DIM])
        x_sb.append(one_token)

    words_i32 = w_words_in.bitcast(I32).rearrange("g p n -> p g n")
    scales_i32 = w_scales_in.bitcast(I32).rearrange("g q n -> q g n")
    w_words = {}
    for c in loads:
        w_words[c] = keep.tile([P, PASSES, 2 * BANK], U8, align_bytes=64, name="w_words%d" % c)

    def load_unit(c):
        nc.sync.dma_start(
            out=w_words[c][:].bitcast(I32), in_=words_i32[:, :, c // 2 : (c + BANK) // 2]
        )
        for r in range(4):
            nc.sync.dma_start(
                out=w_scales[c][:].bitcast(I32)[r:P:32, :, :],
                in_=scales_i32[r:16:4, :, c // 4 : (c + BANK) // 4],
            )

    for c in loads[:LOADS_AHEAD]:
        load_unit(c)
    return x_sb, f_sb, w_words, w_scales, loads[LOADS_AHEAD:], load_unit


def load_sine_table(nc, head):
    zeros = head.tile([P, 1], F32)
    nc.gpsimd.memset(zeros[:], 0.0)
    unused = head.tile([P, 1], F32)
    nc.scalar.activation(out=unused[:], in_=zeros[:], func=ACT.Sin)


def rope_tables(nc, keep, head, f_sb):
    by_token = f_sb[:].rearrange("p a (j y i) -> p j a y i", j=TOK, y=2)
    one_head = head.tile([P, TOK, 3, 2, 2, HALF], F32)
    for y in range(2):
        nc.scalar.activation(
            out=one_head[:, :, :, y, y, :],
            in_=by_token[:, :, :, y, :],
            func=ACT.Sin,
            bias=math.pi / 2,
        )
        nc.scalar.activation(
            out=one_head[:, :, :, y, 1 - y, :],
            in_=by_token[:, :, :, y, :],
            func=ACT.Sin,
            scale=(-1.0 if y == 0 else 1.0),
        )
    return one_head


def spread_factors(copy, table, one_head, j):
    copy(
        out=table[:, j, :, :],
        in_=one_head[:, j].rearrange("p a y s i -> p (a y s i)")
        .unsqueeze(1)
        .to_broadcast([P, PERIODS, 2 * HEAD]),
    )


def keep_busy(nc, psum, zeros, n):
    unread = psum.tile([P, BANK], F32, tag="bank")
    for i in range(n):
        nc.tensor.matmul(out=unread[:], lhsT=zeros[:, 0:P], rhs=zeros[:], start=True, stop=True)


def quantise_x(nc, keep, head, psum, x_sb, ident, zeros, table, one_head):
    tiles = TOK * PASSES
    grouped = head.tile([P, tiles, 4 * P], BF16, align_bytes=64)
    x_codes = keep.tile([P, tiles, P], U32, align_bytes=64)
    x_scales = keep.tile([P, tiles, P], U8, align_bytes=64)

    def quantise(m):
        nc.vector.quantize_mx(
            out=x_codes[:, m : m + 2, :].rearrange("p a r -> p (a r)").bitcast(FP8X4),
            scales=x_scales[:, m : m + 2, :].rearrange("p a r -> p (a r)"),
            in_=grouped[:, m : m + 2, :].rearrange("p a c -> p (a c)"),
        )

    keep_busy(nc, psum, zeros, WARM_UP)
    for m in range(0, tiles, 2):
        if m == tiles // 2:
            keep_busy(nc, psum, zeros, STAY_WARM)
        flipped = psum.tile([P, 4, P], F32, tag="bank")
        for a in range(2):
            j, g = divmod(m + a, PASSES)
            words = x_sb[j][:].bitcast(F32)
            for u in range(2):
                nc.tensor.transpose(
                    flipped[:, 2 * a + u, :],
                    words[:, 256 * g + u : 256 * (g + 1) : 2],
                    ident[:],
                )
        side_by_side = grouped[:, m : m + 2, :].bitcast(F32).rearrange("p a (r u) -> p a r u", u=2)
        pairs = flipped[:].rearrange("p (a u) r -> p a r u", u=2)
        nc.scalar.copy(out=side_by_side, in_=pairs)
        if m > 0:
            quantise(m - 2)
        if m // 2 < TOK - 1:
            spread_factors(nc.vector.tensor_copy, table, one_head, m // 2)
    quantise(tiles - 2)
    spread_factors(nc.scalar.copy, table, one_head, TOK - 1)
    return x_codes, x_scales


def tile_attention_pa_kernel(
    tc, x, f1, f2, f3, Wqkv_words, Wqkv_scales, out_0, out_1, out_2
):
    nc = tc.nc
    outs = (out_0, out_1, out_2)
    with ExitStack() as ctx:
        keep = ctx.enter_context(tc.tile_pool(name="keep", bufs=1))
        psum = ctx.enter_context(tc.psum_pool(name="psum", bufs=8))

        ctx.enter_context(tc.manual_schedule())

        prods = {}
        for third in range(2):
            prods[third] = keep.tile(
                [P, TOK, THIRD // GROUP, 2, GROUP], F32, name="prod%d" % third
            )
        v_sb = keep.tile([P, HEADS, TOK, HEAD], F32)

        order = bank_order()
        with tc.tile_pool(name="head", bufs=1) as head:
            idle_operand = head.tile([P, BANK], BF16)
            nc.vector.memset(idle_operand[:], 0.0)
            load_sine_table(nc, head)
            ident = head.tile([P, P], F32)
            make_identity(nc, ident[:])
            x_sb, f_sb, w_words, w_scales, later_loads, load_unit = load_inputs(
                nc, keep, head, x, (f1, f2, f3), Wqkv_words, Wqkv_scales, order
            )
            one_head = rope_tables(nc, keep, head, f_sb)
            periods = keep.tile([P, TOK, PERIODS, 2 * HEAD], F32)
            x_codes, x_scales = quantise_x(
                nc, keep, head, psum, x_sb, ident, idle_operand, periods, one_head
            )
            table = periods[:].rearrange("p j r (a c) -> p j (r a) c", c=2 * GROUP)

        results = ctx.enter_context(tc.tile_pool(name="results", bufs=4))

        def project(c, j):
            acc = psum.tile([P, BANK], F32, tag="bank")
            for g in range(PASSES):
                nc.tensor.matmul_mx(
                    out=acc[:],
                    lhsT=x_codes[:, PASSES * j + g, :].bitcast(FP8X4),
                    lhsT_scale=x_scales[:, PASSES * j + g, :],
                    rhs=w_words[c][:, g, :].bitcast(FP4X4),
                    rhs_scale=w_scales[c][:, g, :],
                    start=(g == 0),
                    stop=(g == PASSES - 1),
                )
            return acc

        def products(acc, prod, j, bank):
            first = bank * BANK_GROUPS
            window = first % 3
            nc.vector.tensor_tensor(
                out=prod[:, j, first : first + BANK_GROUPS, :, :],
                in0=acc[:]
                .rearrange("p (g c) -> p g c", c=GROUP)
                .unsqueeze(2)
                .to_broadcast([P, BANK_GROUPS, 2, GROUP]),
                in1=table[:, j, window : window + BANK_GROUPS, :].rearrange(
                    "p g (y c) -> p g y c", y=2
                ),
                op=ALU.mult,
            )

        def add_products(engine, prod, result, h0, j0, j1):
            h1 = h0 + result.shape[1]
            halves = prod[:, j0:j1, 3 * h0 : 3 * h1, :, :].rearrange(
                "p j (h a) y (s i) -> p j h (a y) s i", a=3, s=2
            )
            engine.tensor_tensor(
                out=result[:, :, j0:j1, :].rearrange("p h j (a i) -> p j h a i", i=HALF),
                in0=halves[:, :, :, :, 0, :],
                in1=halves[:, :, :, :, 1, :],
                op=ALU.add,
            )

        def store(queue, rows, third, h, j0=0, j1=TOK):
            queue.dma_start(
                out=outs[third][:, h].rearrange("b (p j) d -> p b (j d)", j=TOK)[
                    :, :, j0 * HEAD : j1 * HEAD
                ],
                in_=rows[:, j0:j1, :].rearrange("p j d -> p (j d)"),
            )

        def copy_v(acc, c0, j):
            lead = (HEAD - c0 % HEAD) % HEAD
            whole = (BANK - lead) // HEAD
            rest = BANK - lead - whole * HEAD
            ha = (c0 + lead) // HEAD
            if lead:
                nc.scalar.copy(out=v_sb[:, ha - 1, j, HEAD - lead :], in_=acc[:, 0:lead])
            nc.scalar.copy(
                out=v_sb[:, ha : ha + whole, j, :],
                in_=acc[:, lead : lead + whole * HEAD].rearrange("p (h d) -> p h d", d=HEAD),
            )
            if rest:
                nc.scalar.copy(out=v_sb[:, ha + whole, j, 0:rest], in_=acc[:, BANK - rest :])

        result = None
        waiting = []
        for step, (third, bank, j) in enumerate(order + [(None, 0, 0)] * (STORE_LAG + 2)):
            while waiting and waiting[0][0] <= step:
                store(nc.sync, waiting[0][1], waiting[0][2], waiting[0][3])
                waiting = waiting[1:]
            if third is None:
                continue
            c0 = bank * BANK
            h0, h1 = c0 // HEAD, (c0 + BANK) // HEAD
            acc = project(third * THIRD + c0, j)
            if third == 2:
                copy_v(acc, c0, j)
                if bank == 1 and j % 2 == 1:
                    for h in range(h0, h1):
                        store(nc.sync, v_sb[:, h], third, h, j - 1, j + 1)
                elif bank != 1 and j == TOK - 1:
                    for h in range(h0, h1):
                        store(nc.sync, v_sb[:, h], third, h)
            elif (third, bank) == (1, THIRD_BANKS - 1):
                products(acc, prods[third], j, bank)
                if j == TOK - 1:
                    for h in range(h0, h1, 2):
                        pair = results.tile([P, 2, TOK, HEAD], F32, tag="last", bufs=3)
                        add_products(nc.vector, prods[third], pair, h, 0, TOK)
                        for k in range(2):
                            waiting.append(
                                (step + STORE_LAG - 1 + (h - h0) // 2, pair[:, k], third, h + k)
                            )
            else:
                if j == 0:
                    result = results.tile([P, h1 - h0, TOK, HEAD], F32, tag="result")
                products(acc, prods[third], j, bank)
                if j == 1:
                    add_products(nc.gpsimd, prods[third], result, h0, 0, 2)
                if j == TOK - 1:
                    lot = 3 if bank == THIRD_BANKS - 1 else h1 - h0
                    for h in range(h0, h1, lot):
                        n = min(lot, h1 - h)
                        add_products(
                            nc.gpsimd, prods[third], result[:, h - h0 : h - h0 + n], h, 2, TOK
                        )
                        for k in range(h, h + n):
                            waiting.append((step + STORE_LAG + (h - h0) // 3, result[:, k - h0], third, k))
